import numpy as np
import ml_dtypes


def mxq(x, axis, fmt="e4m3"):
    dtype, down = {"e4m3": (ml_dtypes.float8_e4m3fn, 7), "e5m2": (ml_dtypes.float8_e5m2, 14)}[fmt]
    v = np.moveaxis(np.asarray(x, np.float32).astype(ml_dtypes.bfloat16).astype(np.float64), axis, -1)
    blocks = v.reshape(v.shape[:-1] + (-1, 32))
    amax = np.abs(blocks).max(-1, keepdims=True)
    byte = np.maximum(np.where(amax > 0, np.frexp(amax)[1] - 1 + 127, 0) - down, 1)
    scale = np.exp2(byte - 127.0)
    codes = (blocks / scale).astype(np.float32).astype(dtype).astype(np.float64)
    return np.moveaxis((codes * scale).reshape(v.shape), -1, axis)


WIDE = False


def mx_kscale(k):
    if not WIDE:
        return np.ones(k)
    levels = np.array([10, -10, 5, -5, 0])
    a = np.random.permutation(np.resize(levels, k // 512 * 4)).reshape(k // 512, 4)
    idx = np.arange(k)
    return np.exp2(a[idx // 512, idx % 128 // 32])


BF16 = ml_dtypes.bfloat16


def bf(x):
    return np.asarray(x, np.float32).astype(BF16)


def f64(x):
    return np.asarray(x).astype(np.float64)


B, N, H = 1, 1536, 512
BN_EPS = 1e-5


def setup_inputs():
    s = mx_kscale(H)
    return {"h": bf(np.random.standard_normal((B, N, H)) * s),
            "adj": bf(np.random.random_sample((B, N, N))),
            "W": bf(np.random.standard_normal((H, H)) * 2.0 / np.sqrt(H) / s[None, :]),
            "b": bf(np.random.standard_normal(H) * 1.0),
            "bn_weight": bf(1.0 + 0.1 * np.random.standard_normal(H)),
            "bn_bias": bf(0.1 * np.random.standard_normal(H)),
            "res_weight": bf((0.3 + 0.1 * np.random.standard_normal(1)) / s.max())}


def reference(h, adj, W, b, bn_weight, bn_bias, res_weight):
    h = f64(h)
    A = f64(adj) + np.eye(N)
    deg = A.sum(axis=-1)
    dis = deg ** -0.5
    dis = np.where(np.isinf(dis), 0.0, dis)
    A_hat = dis[:, :, None] * A * dis[:, None, :]
    h_lin = (mxq(h, 2, "e4m3") @ mxq(f64(W), 1, "e4m3").T) + f64(b)
    out = mxq(A_hat, 2, "e4m3") @ mxq(h_lin, 1, "e4m3")
    flat = out.reshape(B * N, H)
    mean = flat.mean(axis=0)
    var = flat.var(axis=0)
    flat = (flat - mean) * (1.0 / np.sqrt(var + BN_EPS)) * f64(bn_weight) + f64(bn_bias)
    out = flat.reshape(B, N, H)
    out = np.maximum(out, 0.0)
    return out + f64(res_weight) * h

@@ -1,0 +1,461 @@
+from contextlib import ExitStack
+
+import concourse.mybir as mybir
+from concourse.masks import make_identity
+
+F32 = mybir.dt.float32
+BF16 = mybir.dt.bfloat16
+U8 = mybir.dt.uint8
+U32 = mybir.dt.uint32
+FP8X4 = mybir.dt.float8_e4m3fn_x4
+ALU = mybir.AluOpType
+ACT = mybir.ActivationFunctionType
+
+P = 128
+NODES = 1536
+FEAT = 512
+NT = NODES // P
+NG = NODES // 512
+NJ = FEAT // P
+BN_EPS = 1e-5
+TINY = 1e-30
+PINNED = True
+
+FLOPS = 2 * NODES * FEAT * FEAT + 2 * NODES * NODES * FEAT
+
+
+def tile_gcnlayer_kernel(tc, h, adj, W, b, bn_weight, bn_bias, res_weight, out):
+    nc = tc.nc
+    with ExitStack() as ctx:
+        if PINNED:
+            ctx.enter_context(tc.manual_schedule())
+        const = ctx.enter_context(tc.tile_pool(name="const", bufs=1))
+        keep = ctx.enter_context(tc.tile_pool(name="keep", bufs=1))
+        hlgp = ctx.enter_context(tc.tile_pool(name="hlgp", bufs=2))
+        fpool = ctx.enter_context(tc.tile_pool(name="fpool", bufs=3))
+        gpool = ctx.enter_context(tc.tile_pool(name="gpool", bufs=3))
+        opool = ctx.enter_context(tc.tile_pool(name="opool", bufs=4))
+        ring = ctx.enter_context(tc.psum_pool(name="ring", bufs=4))
+        ybank = ctx.enter_context(tc.psum_pool(name="ybank", bufs=1))
+
+        h_v = h.rearrange("o (w q e) k -> q (o w) e k", q=P, e=2)
+        adj_v = adj.rearrange("o (w q e) n -> q (o w) e n", q=P, e=2)
+        out_v = out.rearrange("o (w q e) f -> q (o w) e f", q=P, e=2)
+
+        w_sb = keep.tile([P, NJ * FEAT], BF16, name="w_sb")
+        nc.sync.dma_start(
+            out=w_sb[:].rearrange("q (r k) -> q r k", r=NJ),
+            in_=W.rearrange("(r q) k -> q r k", q=P),
+        )
+        h_sb = keep.tile([P, NT * FEAT], BF16, name="h_sb")
+        for g in range(NG):
+            nc.sync.dma_start(
+                out=h_sb[:, 2048 * g : 2048 * g + 2048].rearrange("q (w x) -> q w x", w=2),
+                in_=h_v[:, 2 * g : 2 * g + 2, :, :].rearrange("q w e k -> q w (e k)"),
+            )
+        a_sb = keep.tile([P, NT * NODES], BF16, name="a_sb")
+        for w in range(NT // 2):
+            nc.sync.dma_start(
+                out=a_sb[:, 2 * NODES * w : 2 * NODES * (w + 1)],
+                in_=adj_v[:, w, :, :].rearrange("q e n -> q (e n)"),
+            )
+        a32 = a_sb[:].bitcast(F32)
+
+        one1 = const.tile([P, 1], F32, name="one1")
+        nc.vector.memset(one1[:], 1.0)
+        junk = const.tile([P, 1], F32, name="junk")
+        nc.scalar.activation(out=junk[:], in_=one1[:], func=ACT.Sqrt)
+        ident_f = const.tile([P, P], F32, name="ident_f")
+        make_identity(nc, ident_f[:])
+        ident_b = const.tile([P, P], BF16, name="ident_b")
+        make_identity(nc, ident_b[:])
+        ones = const.tile([P, P], BF16, name="ones")
+        nc.vector.memset(ones[:], 1.0)
+        zb = const.tile([P, FEAT], BF16, name="zb")
+        nc.vector.memset(zb[:], 0.0)
+        vt = const.tile([P, P], BF16, name="vt")
+        nc.vector.memset(vt[:], 0.0)
+        nc.scalar.dma_start(out=zb[0:1, :], in_=b.rearrange("(o f) -> o f", o=1))
+        nc.scalar.dma_start(out=vt[0:4, :], in_=bn_weight.rearrange("(j p) -> j p", p=P))
+        nc.scalar.dma_start(out=vt[4:8, :], in_=bn_bias.rearrange("(j p) -> j p", p=P))
+        res_b = const.tile([P, 1], BF16, name="res_b")
+        nc.scalar.dma_start(out=res_b[:], in_=res_weight.partition_broadcast(P))
+
+        bb_ps = ring.tile([P, FEAT], F32, name="bb_ps", tag="ring")
+        nc.tensor.matmul(out=bb_ps[:], lhsT=ones[:], rhs=zb[:], start=True, stop=True)
+        b_bc = const.tile([P, FEAT], BF16, name="b_bc")
+        nc.scalar.copy(out=b_bc[:], in_=bb_ps[:])
+        vt_ps = ring.tile([P, P], BF16, name="vt_ps", tag="ring")
+        nc.tensor.transpose(vt_ps[:], vt[:], ident_b[:])
+        gb = const.tile([P, 8], F32, name="gb")
+        nc.vector.tensor_copy(out=gb[:], in_=vt_ps[:, 0:8])
+        res_f = const.tile([P, 1], F32, name="res_f")
+        nc.vector.tensor_copy(out=res_f[:], in_=res_b[:])
+
+        def words_to_k(src32, pair, grouped32):
+            xt = ring.tile([P, 512], F32, name="xt", tag="ring")
+            for r2 in range(2):
+                for u in range(2):
+                    lo = 256 * (2 * pair + r2) + 128 * u
+                    nc.tensor.transpose(
+                        xt[:, 256 * r2 + 128 * u : 256 * r2 + 128 * u + 128],
+                        src32[:, lo : lo + 128],
+                        ident_f[:],
+                    )
+            nc.scalar.copy(
+                out=grouped32[:, 512 * pair : 512 * pair + 512].rearrange(
+                    "p (r q u) -> p r q u", r=2, u=2
+                ),
+                in_=xt[:].rearrange("p (r u q) -> p r q u", r=2, u=2),
+            )
+
+        wg = keep.tile([P, 4 * FEAT], BF16, name="wg", align_bytes=64)
+        w_codes = keep.tile([P, FEAT], U32, name="w_codes", align_bytes=64)
+        w_sc = keep.tile([P, FEAT], U8, name="w_sc", align_bytes=64)
+        hg = keep.tile([P, 4 * NODES], BF16, name="hg", align_bytes=64)
+        h_codes = keep.tile([P, NODES], U32, name="h_codes", align_bytes=64)
+        h_sc = keep.tile([P, NODES], U8, name="h_sc", align_bytes=64)
+        for pair in range(2):
+            words_to_k(w_sb[:].bitcast(F32), pair, wg[:].bitcast(F32))
+        nc.vector.quantize_mx(out=w_codes[:].bitcast(FP8X4), scales=w_sc[:], in_=wg[:])
+        for g in range(NG):
+            for pair in (2 * g, 2 * g + 1):
+                words_to_k(h_sb[:].bitcast(F32), pair, hg[:].bitcast(F32))
+            nc.vector.quantize_mx(
+                out=h_codes[:, 512 * g : 512 * g + 512].bitcast(FP8X4),
+                scales=h_sc[:, 512 * g : 512 * g + 512],
+                in_=hg[:, 2048 * g : 2048 * g + 2048],
+            )
+
+        r_sb = keep.tile([P, NT * FEAT], F32, name="r_sb")
+        for i in range(NT):
+            nc.gpsimd.tensor_scalar(
+                out=r_sb[:, 512 * i : 512 * i + 512],
+                in0=h_sb[:, 512 * i : 512 * i + 512],
+                scalar1=res_f[:, 0:1],
+                scalar2=0.0,
+                op0=ALU.mult,
+                op1=ALU.add,
+            )
+
+        hl_codes = keep.tile([P, NG * FEAT], U32, name="hl_codes", align_bytes=64)
+        hl_sc = keep.tile([P, NG * FEAT], U8, name="hl_sc", align_bytes=64)
+        hlgs = {}
+
+        def stage1_piece(k):
+            g, fc = k // NJ, k % NJ
+            if fc == 0:
+                hlgs[g] = hlgp.tile([P, 4 * FEAT], BF16, name="hlg", tag="hlg", align_bytes=64)
+            yb = ybank.tile([P, 512], F32, name="y%d" % fc, tag="y%d" % fc)
+            for t in range(4):
+                i = 4 * g + t
+                nc.tensor.matmul_mx(
+                    out=yb[:, 128 * t : 128 * t + 128],
+                    lhsT=h_codes[:, 128 * i : 128 * i + 128].bitcast(FP8X4),
+                    lhsT_scale=h_sc[:, 128 * i : 128 * i + 128],
+                    rhs=w_codes[:, 128 * fc : 128 * fc + 128].bitcast(FP8X4),
+                    rhs_scale=w_sc[:, 128 * fc : 128 * fc + 128],
+                    start=True,
+                    stop=True,
+                )
+            nc.vector.tensor_tensor(
+                out=hlgs[g][:, 512 * fc : 512 * fc + 512].rearrange("p (f t) -> p f t", t=4),
+                in0=yb[:].rearrange("p (t f) -> p f t", t=4),
+                in1=b_bc[:, 128 * fc : 128 * fc + 128].unsqueeze(2).to_broadcast([P, 128, 4]),
+                op=ALU.add,
+            )
+            if fc == NJ - 1:
+                nc.vector.quantize_mx(
+                    out=hl_codes[:, 512 * g : 512 * g + 512].bitcast(FP8X4),
+                    scales=hl_sc[:, 512 * g : 512 * g + 512],
+                    in_=hlgs[g][:],
+                )
+
+        zs = keep.tile([P, NJ, NODES], F32, name="zs")
+        junk_s = zs[:, 0, 0 : NODES // 2].bitcast(BF16)
+        junk_v = zs[:, 1, 0 : NODES // 2].bitcast(BF16)
+        deg_s = const.tile([P, NT // 2], F32, name="deg_s")
+        deg_v = const.tile([P, NT // 2], F32, name="deg_v")
+        d1 = const.tile([P, NT], F32, name="d1")
+        sq = const.tile([P, NT], F32, name="sq")
+        rc = const.tile([P, NT], F32, name="rc")
+        dis = const.tile([P, NT], F32, name="dis")
+        d_sb = keep.tile([P, NODES], F32, name="d_sb")
+        ee = keep.tile([P, NT, P], F32, name="ee")
+
+        def row_sums(w):
+            nc.scalar.activation(
+                out=junk_s,
+                in_=a_sb[:, NODES * 2 * w : NODES * (2 * w + 1)],
+                func=ACT.Copy,
+                accum_out=deg_s[:, w : w + 1],
+            )
+            nc.vector.tensor_scalar(
+                out=junk_v,
+                in0=a_sb[:, NODES * (2 * w + 1) : NODES * (2 * w + 2)],
+                scalar1=1.0,
+                scalar2=None,
+                op0=ALU.mult,
+                op1=ALU.add,
+                accum_out=deg_v[:, w : w + 1],
+            )
+
+        def dis_a(gq):
+            d1v = d1[:, 4 * gq : 4 * gq + 4].rearrange("p (w e) -> p w e", e=2)
+            for e, deg in ((0, deg_s), (1, deg_v)):
+                nc.vector.tensor_scalar(
+                    out=d1v[:, :, e],
+                    in0=deg[:, 2 * gq : 2 * gq + 2],
+                    scalar1=1.0,
+                    scalar2=TINY,
+                    op0=ALU.add,
+                    op1=ALU.max,
+                )
+
+        def dis_b(gq):
+            gs = slice(4 * gq, 4 * gq + 4)
+            nc.scalar.activation(out=sq[:, gs], in_=d1[:, gs], func=ACT.Sqrt)
+
+        def dis_c(gq):
+            gs = slice(4 * gq, 4 * gq + 4)
+            nc.vector.reciprocal(out=rc[:, gs], in_=sq[:, gs])
+            nc.vector.scalar_tensor_tensor(
+                out=dis[:, gs],
+                in0=d1[:, gs],
+                scalar=2.0 * TINY,
+                in1=rc[:, gs],
+                op0=ALU.is_gt,
+                op1=ALU.mult,
+            )
+            for t in range(4):
+                i = 4 * gq + t
+                nc.gpsimd.tensor_scalar(
+                    out=ee[:, i, :],
+                    in0=ident_f[:],
+                    scalar1=dis[:, i : i + 1],
+                    scalar2=0.0,
+                    op0=ALU.mult,
+                    op1=ALU.add,
+                )
+
+        dps = {}
+
+        def spread_matmuls(gq):
+            if gq == 0:
+                dp = ring.tile([P, 512], F32, name="dp", tag="ring")
+            else:
+                dp = ybank.tile([P, 512], F32, name="dpy%d" % gq, tag="y%d" % (gq - 1))
+            dps[gq] = dp
+            for t in range(4):
+                nc.tensor.matmul(
+                    out=dp[:, 128 * t : 128 * t + 128],
+                    lhsT=dis[:, 4 * gq + t : 4 * gq + t + 1].to_broadcast([P, P]),
+                    rhs=ident_f[:],
+                    start=True,
+                    stop=True,
+                )
+
+        def spread_copy(gq):
+            nc.scalar.copy(out=d_sb[:, 512 * gq : 512 * gq + 512], in_=dps[gq][:])
+
+        a_codes = keep.tile([P, NG, NODES], U32, name="a_codes", align_bytes=64)
+        a_sc = keep.tile([P, NG, NODES], U8, name="a_sc", align_bytes=64)
+        st = const.tile([P, NJ, NG, 6], F32, name="st")
+        tus, fts, grps, ybs = {}, {}, {}, {}
+
+        def unit_transposes(c, g):
+            tus[(c, g)] = []
+            for u in range(2):
+                tu = ring.tile([P, 512], F32, name="tu", tag="ring")
+                for t in range(4):
+                    lo = 768 * (4 * c + t) + 128 * (2 * g + u)
+                    nc.tensor.transpose(
+                        tu[:, 128 * t : 128 * t + 128], a32[:, lo : lo + 128], ident_f[:]
+                    )
+                tus[(c, g)].append(tu)
+
+        def unit_planes(c, g):
+            f_t = fpool.tile([P, 4, 512], F32, name="f_t", tag="f_t")
+            fts[(c, g)] = f_t
+            for t in range(4):
+                u, e = t // 2, t % 2
+                nc.scalar.activation(
+                    out=f_t[:, t, :],
+                    in_=tus[(c, g)][u][:].bitcast(BF16).rearrange("p (m e) -> p m e", e=2)[:, :, e],
+                    func=ACT.Copy,
+                    scale=dis[:, 4 * g + t : 4 * g + t + 1],
+                )
+            if c == g:
+                for t in range(4):
+                    nc.gpsimd.tensor_tensor(
+                        out=f_t[:, t, 128 * t : 128 * t + 128],
+                        in0=f_t[:, t, 128 * t : 128 * t + 128],
+                        in1=ee[:, 4 * g + t, :],
+                        op=ALU.add,
+                    )
+
+        def unit_scale(c, g):
+            cs = slice(512 * c, 512 * c + 512)
+            grp = gpool.tile([P, 2048], BF16, name="grp", tag="grp", align_bytes=64)
+            grps[(c, g)] = grp
+            nc.vector.tensor_tensor(
+                out=grp[:].rearrange("p (m t) -> p m t", t=4),
+                in0=fts[(c, g)][:].rearrange("p t m -> p m t"),
+                in1=d_sb[:, cs].unsqueeze(2).to_broadcast([P, 512, 4]),
+                op=ALU.mult,
+            )
+
+        def unit_quant(c, g):
+            cs = slice(512 * c, 512 * c + 512)
+            nc.vector.quantize_mx(
+                out=a_codes[:, g, cs].bitcast(FP8X4), scales=a_sc[:, g, cs], in_=grps[(c, g)][:]
+            )
+
+        def unit_matmuls(c, g):
+            cs = slice(512 * c, 512 * c + 512)
+            if g == 0:
+                ybs[c] = [
+                    ybank.tile([P, 512], F32, name="y%d" % j, tag="y%d" % j) for j in range(NJ)
+                ]
+            for j in range(NJ):
+                lo = 512 * g + 128 * j
+                nc.tensor.matmul_mx(
+                    out=ybs[c][j][:],
+                    lhsT=hl_codes[:, lo : lo + 128].bitcast(FP8X4),
+                    lhsT_scale=hl_sc[:, lo : lo + 128],
+                    rhs=a_codes[:, g, cs].bitcast(FP8X4),
+                    rhs_scale=a_sc[:, g, cs],
+                    start=(g == 0),
+                    stop=(g == NG - 1),
+                )
+
+        def chunk_stats(c):
+            for j in range(NJ):
+                nc.vector.bn_stats(out=st[:, j, c, :], in_=ybs[c][j][:])
+
+        def chunk_copy(c):
+            cs = slice(512 * c, 512 * c + 512)
+            for j in range(NJ):
+                nc.scalar.copy(out=zs[:, j, cs], in_=ybs[c][j][:])
+
+        units = [(c, g) for c in range(NG) for g in range(NG)]
+        last = len(units) - 1
+        stage1_piece(0)
+        stage1_piece(1)
+        for w in range(NT // 2):
+            row_sums(w)
+            if w == 2:
+                dis_a(0)
+            if w == 3:
+                dis_b(0)
+            stage1_piece(2 + w)
+            if w == 1:
+                unit_transposes(0, 0)
+            if w == 3:
+                dis_c(0)
+                spread_matmuls(0)
+        spread_copy(0)
+        unit_transposes(0, 1)
+        dis_a(1)
+        dis_a(2)
+        unit_planes(0, 0)
+        dis_b(1)
+        dis_b(2)
+        stage1_piece(8)
+        stage1_piece(9)
+        dis_c(1)
+        dis_c(2)
+        stage1_piece(10)
+        stage1_piece(11)
+        spread_matmuls(1)
+        spread_matmuls(2)
+        held = None
+        for k, (c, g) in enumerate(units):
+            if k > 0:
+                unit_planes(c, g)
+            if k == 1:
+                spread_copy(1)
+                spread_copy(2)
+            copied = k >= 3 and units[k - 3][1] == NG - 1
+            if copied:
+                chunk_copy(units[k - 3][0])
+            if k == last:
+                unit_quant(*units[k - 1])
+            unit_scale(c, g)
+            if k >= 2 and units[k - 2][1] == NG - 1:
+                chunk_stats(units[k - 2][0])
+            if copied and held is not None:
+                unit_matmuls(*held)
+                held = None
+            if k + 2 <= last:
+                unit_transposes(*units[k + 2])
+            if k >= 1:
+                if k < last:
+                    unit_quant(*units[k - 1])
+                if units[k - 1][1] == 0 and units[k - 1][0] > 0:
+                    held = units[k - 1]
+                else:
+                    unit_matmuls(*units[k - 1])
+        unit_quant(*units[last])
+        unit_matmuls(*units[last])
+        chunk_stats(NG - 1)
+
+        mv = const.tile([P, NJ, 2], F32, name="mv")
+        for j in range(NJ):
+            nc.vector.bn_aggr(out=mv[:, j, :], in_=st[:, j, :, :].rearrange("p c s -> p (c s)"))
+        ve = const.tile([P, NJ], F32, name="ve")
+        nc.vector.tensor_scalar(out=ve[:], in0=mv[:, :, 1], scalar1=BN_EPS, scalar2=None, op0=ALU.add)
+        sd = const.tile([P, NJ], F32, name="sd")
+        nc.scalar.activation(out=sd[:], in_=ve[:], func=ACT.Sqrt)
+        rs = const.tile([P, NJ], F32, name="rs")
+        nc.vector.reciprocal(out=rs[:], in_=sd[:])
+        sc = const.tile([P, NJ], F32, name="sc")
+        nc.vector.tensor_tensor(out=sc[:], in0=gb[:, 0:4], in1=rs[:], op=ALU.mult)
+        ms = const.tile([P, NJ], F32, name="ms")
+        nc.vector.tensor_tensor(out=ms[:], in0=mv[:, :, 0], in1=sc[:], op=ALU.mult)
+        sh = const.tile([P, NJ], F32, name="sh")
+        nc.vector.tensor_tensor(out=sh[:], in0=gb[:, 4:8], in1=ms[:], op=ALU.subtract)
+
+        def normalise(c, j, eng):
+            cs = slice(512 * c, 512 * c + 512)
+            if eng == "S":
+                nc.scalar.activation(
+                    out=zs[:, j, cs],
+                    in_=(zs[:, j, cs] if c < NG - 1 else ybs[c][j][:]),
+                    func=ACT.Identity,
+                    scale=sc[:, j : j + 1],
+                    bias=sh[:, j : j + 1],
+                )
+            else:
+                (nc.vector if eng == "V" else nc.gpsimd).tensor_scalar(
+                    out=zs[:, j, cs],
+                    in0=zs[:, j, cs],
+                    scalar1=sc[:, j : j + 1],
+                    scalar2=sh[:, j : j + 1],
+                    op0=ALU.mult,
+                    op1=ALU.add,
+                )
+
+        normalise(0, 0, "S")
+        for j in range(1, NJ):
+            normalise(0, j, "V")
+        for j in range(NJ):
+            normalise(1, j, "G")
+            normalise(2, j, "S")
+
+        for i in range(NT):
+            ob = ring.tile([P, FEAT], F32, name="ob", tag="ring")
+            for j in range(NJ):
+                nc.tensor.transpose(
+                    ob[:, 128 * j : 128 * j + 128], zs[:, j, 128 * i : 128 * i + 128], ident_f[:]
+                )
+            o_sb = opool.tile([P, FEAT], F32, name="o_sb", tag="o_sb")
+            nc.vector.scalar_tensor_tensor(
+                out=o_sb[:],
+                in0=ob[:],
+                scalar=0.0,
+                in1=r_sb[:, 512 * i : 512 * i + 512],
+                op0=ALU.max,
+                op1=ALU.add,
+            )
+            nc.sync.dma_start(out=out_v[:, i // 2, i % 2, :], in_=o_sb[:])

@@ -61,10 +61,6 @@ def tile_gcnlayer_kernel(tc, h, adj, W, b, bn_weight, bn_bias, res_weight, out):
             )
         a32 = a_sb[:].bitcast(F32)
 
-        one1 = const.tile([P, 1], F32, name="one1")
-        nc.vector.memset(one1[:], 1.0)
-        junk = const.tile([P, 1], F32, name="junk")
-        nc.scalar.activation(out=junk[:], in_=one1[:], func=ACT.Sqrt)
         ident_f = const.tile([P, P], F32, name="ident_f")
         make_identity(nc, ident_f[:])
         ident_b = const.tile([P, P], BF16, name="ident_b")
@@ -80,17 +76,23 @@ def tile_gcnlayer_kernel(tc, h, adj, W, b, bn_weight, bn_bias, res_weight, out):
         nc.scalar.dma_start(out=vt[4:8, :], in_=bn_bias.rearrange("(j p) -> j p", p=P))
         res_b = const.tile([P, 1], BF16, name="res_b")
         nc.scalar.dma_start(out=res_b[:], in_=res_weight.partition_broadcast(P))
+        one1 = const.tile([P, 1], F32, name="one1")
+        nc.vector.memset(one1[:], 1.0)
+        junk = const.tile([P, 1], F32, name="junk")
+        nc.scalar.activation(out=junk[:], in_=one1[:], func=ACT.Sqrt)
 
-        bb_ps = ring.tile([P, FEAT], F32, name="bb_ps", tag="ring")
-        nc.tensor.matmul(out=bb_ps[:], lhsT=ones[:], rhs=zb[:], start=True, stop=True)
         b_bc = const.tile([P, FEAT], BF16, name="b_bc")
-        nc.scalar.copy(out=b_bc[:], in_=bb_ps[:])
-        vt_ps = ring.tile([P, P], BF16, name="vt_ps", tag="ring")
-        nc.tensor.transpose(vt_ps[:], vt[:], ident_b[:])
         gb = const.tile([P, 8], F32, name="gb")
-        nc.vector.tensor_copy(out=gb[:], in_=vt_ps[:, 0:8])
         res_f = const.tile([P, 1], F32, name="res_f")
-        nc.vector.tensor_copy(out=res_f[:], in_=res_b[:])
+
+        def small_vectors():
+            bb_ps = ring.tile([P, FEAT], F32, name="bb_ps", tag="ring")
+            nc.tensor.matmul(out=bb_ps[:], lhsT=ones[:], rhs=zb[:], start=True, stop=True)
+            nc.scalar.copy(out=b_bc[:], in_=bb_ps[:])
+            vt_ps = ring.tile([P, P], BF16, name="vt_ps", tag="ring")
+            nc.tensor.transpose(vt_ps[:], vt[:], ident_b[:])
+            nc.vector.tensor_copy(out=gb[:], in_=vt_ps[:, 0:8])
+            nc.vector.tensor_copy(out=res_f[:], in_=res_b[:])
 
         def words_to_k(src32, pair, grouped32):
             xt = ring.tile([P, 512], F32, name="xt", tag="ring")
@@ -126,17 +128,8 @@ def tile_gcnlayer_kernel(tc, h, adj, W, b, bn_weight, bn_bias, res_weight, out):
                 scales=h_sc[:, 512 * g : 512 * g + 512],
                 in_=hg[:, 2048 * g : 2048 * g + 2048],
             )
-
-        r_sb = keep.tile([P, NT * FEAT], F32, name="r_sb")
-        for i in range(NT):
-            nc.gpsimd.tensor_scalar(
-                out=r_sb[:, 512 * i : 512 * i + 512],
-                in0=h_sb[:, 512 * i : 512 * i + 512],
-                scalar1=res_f[:, 0:1],
-                scalar2=0.0,
-                op0=ALU.mult,
-                op1=ALU.add,
-            )
+            if g == 0:
+                small_vectors()
 
         hl_codes = keep.tile([P, NG * FEAT], U32, name="hl_codes", align_bytes=64)
         hl_sc = keep.tile([P, NG * FEAT], U8, name="hl_sc", align_bytes=64)
@@ -181,7 +174,7 @@ def tile_gcnlayer_kernel(tc, h, adj, W, b, bn_weight, bn_bias, res_weight, out):
         rc = const.tile([P, NT], F32, name="rc")
         dis = const.tile([P, NT], F32, name="dis")
         d_sb = keep.tile([P, NODES], F32, name="d_sb")
-        ee = keep.tile([P, NT, P], F32, name="ee")
+        tmpd = keep.tile([P, NT, P], F32, name="tmpd")
 
         def row_sums(w):
             nc.scalar.activation(
@@ -227,16 +220,34 @@ def tile_gcnlayer_kernel(tc, h, adj, W, b, bn_weight, bn_bias, res_weight, out):
                 op0=ALU.is_gt,
                 op1=ALU.mult,
             )
+
+        dgs = {}
+
+        def diag_matmuls(c):
+            dg = ring.tile([P, 512], F32, name="dg", tag="ring")
+            dgs[c] = dg
             for t in range(4):
-                i = 4 * gq + t
-                nc.gpsimd.tensor_scalar(
-                    out=ee[:, i, :],
-                    in0=ident_f[:],
-                    scalar1=dis[:, i : i + 1],
-                    scalar2=0.0,
-                    op0=ALU.mult,
-                    op1=ALU.add,
+                i = 4 * c + t
+                lo = NODES * i + 256 * (i // 2)
+                nc.tensor.matmul(
+                    out=dg[:, 128 * t : 128 * t + 128],
+                    lhsT=a_sb[:, lo : lo + 256].rearrange("q (p e) -> q p e", e=2)[:, :, i % 2],
+                    rhs=ident_b[:],
+                    start=True,
+                    stop=False,
                 )
+                nc.tensor.matmul(
+                    out=dg[:, 128 * t : 128 * t + 128],
+                    lhsT=ident_b[:],
+                    rhs=ident_b[:],
+                    start=False,
+                    stop=True,
+                )
+
+        def diag_copy(c):
+            nc.scalar.copy(
+                out=tmpd[:, 4 * c : 4 * c + 4, :].rearrange("p t x -> p (t x)"), in_=dgs[c][:]
+            )
 
         dps = {}
 
@@ -287,11 +298,11 @@ def tile_gcnlayer_kernel(tc, h, adj, W, b, bn_weight, bn_bias, res_weight, out):
                 )
             if c == g:
                 for t in range(4):
-                    nc.gpsimd.tensor_tensor(
+                    nc.scalar.activation(
                         out=f_t[:, t, 128 * t : 128 * t + 128],
-                        in0=f_t[:, t, 128 * t : 128 * t + 128],
-                        in1=ee[:, 4 * g + t, :],
-                        op=ALU.add,
+                        in_=tmpd[:, 4 * g + t, :],
+                        func=ACT.Copy,
+                        scale=dis[:, 4 * g + t : 4 * g + t + 1],
                     )
 
         def unit_scale(c, g):
@@ -349,22 +360,27 @@ def tile_gcnlayer_kernel(tc, h, adj, W, b, bn_weight, bn_bias, res_weight, out):
             if w == 3:
                 dis_b(0)
             stage1_piece(2 + w)
-            if w == 1:
+            if w % 2 == 1:
+                diag_matmuls(w // 2)
+            if w % 2 == 0 and w > 0:
+                diag_copy(w // 2 - 1)
+            if w == 2:
                 unit_transposes(0, 0)
             if w == 3:
                 dis_c(0)
                 spread_matmuls(0)
+        diag_copy(2)
         spread_copy(0)
-        unit_transposes(0, 1)
         dis_a(1)
         dis_a(2)
-        unit_planes(0, 0)
         dis_b(1)
         dis_b(2)
+        unit_planes(0, 0)
+        unit_transposes(0, 1)
         stage1_piece(8)
-        stage1_piece(9)
         dis_c(1)
         dis_c(2)
+        stage1_piece(9)
         stage1_piece(10)
         stage1_piece(11)
         spread_matmuls(1)
@@ -422,12 +438,12 @@ def tile_gcnlayer_kernel(tc, h, adj, W, b, bn_weight, bn_bias, res_weight, out):
                 nc.scalar.activation(
                     out=zs[:, j, cs],
                     in_=(zs[:, j, cs] if c < NG - 1 else ybs[c][j][:]),
-                    func=ACT.Identity,
+                    func=ACT.Relu,
                     scale=sc[:, j : j + 1],
                     bias=sh[:, j : j + 1],
                 )
             else:
-                (nc.vector if eng == "V" else nc.gpsimd).tensor_scalar(
+                nc.vector.tensor_scalar(
                     out=zs[:, j, cs],
                     in0=zs[:, j, cs],
                     scalar1=sc[:, j : j + 1],
@@ -435,13 +451,17 @@ def tile_gcnlayer_kernel(tc, h, adj, W, b, bn_weight, bn_bias, res_weight, out):
                     op0=ALU.mult,
                     op1=ALU.add,
                 )
+                nc.vector.tensor_scalar(
+                    out=zs[:, j, cs], in0=zs[:, j, cs], scalar1=0.0, scalar2=None, op0=ALU.max
+                )
 
         normalise(0, 0, "S")
-        for j in range(1, NJ):
-            normalise(0, j, "V")
-        for j in range(NJ):
-            normalise(1, j, "G")
-            normalise(2, j, "S")
+        normalise(0, 1, "S")
+        normalise(0, 2, "V")
+        normalise(0, 3, "V")
+        for c in (1, 2):
+            for j in range(NJ):
+                normalise(c, j, "S")
 
         for i in range(NT):
             ob = ring.tile([P, FEAT], F32, name="ob", tag="ring")
@@ -452,10 +472,10 @@ def tile_gcnlayer_kernel(tc, h, adj, W, b, bn_weight, bn_bias, res_weight, out):
             o_sb = opool.tile([P, FEAT], F32, name="o_sb", tag="o_sb")
             nc.vector.scalar_tensor_tensor(
                 out=o_sb[:],
-                in0=ob[:],
-                scalar=0.0,
-                in1=r_sb[:, 512 * i : 512 * i + 512],
-                op0=ALU.max,
+                in0=h_sb[:, 512 * i : 512 * i + 512],
+                scalar=res_f[:, 0:1],
+                in1=ob[:],
+                op0=ALU.mult,
                 op1=ALU.add,
             )
             nc.sync.dma_start(out=out_v[:, i // 2, i % 2, :], in_=o_sb[:])

@@ -18,7 +18,6 @@ NT = NODES // P
 NG = NODES // 512
 NJ = FEAT // P
 BN_EPS = 1e-5
-TINY = 1e-30
 PINNED = True
 
 FLOPS = 2 * NODES * FEAT * FEAT + 2 * NODES * NODES * FEAT
@@ -79,7 +78,9 @@ def tile_gcnlayer_kernel(tc, h, adj, W, b, bn_weight, bn_bias, res_weight, out):
         one1 = const.tile([P, 1], F32, name="one1")
         nc.vector.memset(one1[:], 1.0)
         junk = const.tile([P, 1], F32, name="junk")
-        nc.scalar.activation(out=junk[:], in_=one1[:], func=ACT.Sqrt)
+        nc.scalar.activation(out=junk[:], in_=one1[:], func=ACT.Abs_reciprocal_sqrt)
+        epsb = const.tile([P, 1], F32, name="epsb")
+        nc.vector.memset(epsb[:], BN_EPS)
 
         b_bc = const.tile([P, FEAT], BF16, name="b_bc")
         gb = const.tile([P, 8], F32, name="gb")
@@ -169,9 +170,6 @@ def tile_gcnlayer_kernel(tc, h, adj, W, b, bn_weight, bn_bias, res_weight, out):
         junk_v = zs[:, 1, 0 : NODES // 2].bitcast(BF16)
         deg_s = const.tile([P, NT // 2], F32, name="deg_s")
         deg_v = const.tile([P, NT // 2], F32, name="deg_v")
-        d1 = const.tile([P, NT], F32, name="d1")
-        sq = const.tile([P, NT], F32, name="sq")
-        rc = const.tile([P, NT], F32, name="rc")
         dis = const.tile([P, NT], F32, name="dis")
         d_sb = keep.tile([P, NODES], F32, name="d_sb")
         tmpd = keep.tile([P, NT, P], F32, name="tmpd")
@@ -193,33 +191,15 @@ def tile_gcnlayer_kernel(tc, h, adj, W, b, bn_weight, bn_bias, res_weight, out):
                 accum_out=deg_v[:, w : w + 1],
             )
 
-        def dis_a(gq):
-            d1v = d1[:, 4 * gq : 4 * gq + 4].rearrange("p (w e) -> p w e", e=2)
+        def dis_group(gq):
+            dv = dis[:, 4 * gq : 4 * gq + 4].rearrange("p (w e) -> p w e", e=2)
             for e, deg in ((0, deg_s), (1, deg_v)):
-                nc.vector.tensor_scalar(
-                    out=d1v[:, :, e],
-                    in0=deg[:, 2 * gq : 2 * gq + 2],
-                    scalar1=1.0,
-                    scalar2=TINY,
-                    op0=ALU.add,
-                    op1=ALU.max,
+                nc.scalar.activation(
+                    out=dv[:, :, e],
+                    in_=deg[:, 2 * gq : 2 * gq + 2],
+                    func=ACT.Abs_reciprocal_sqrt,
+                    bias=one1[:, 0:1],
                 )
-
-        def dis_b(gq):
-            gs = slice(4 * gq, 4 * gq + 4)
-            nc.scalar.activation(out=sq[:, gs], in_=d1[:, gs], func=ACT.Sqrt)
-
-        def dis_c(gq):
-            gs = slice(4 * gq, 4 * gq + 4)
-            nc.vector.reciprocal(out=rc[:, gs], in_=sq[:, gs])
-            nc.vector.scalar_tensor_tensor(
-                out=dis[:, gs],
-                in0=d1[:, gs],
-                scalar=2.0 * TINY,
-                in1=rc[:, gs],
-                op0=ALU.is_gt,
-                op1=ALU.mult,
-            )
 
         dgs = {}
 
@@ -355,10 +335,8 @@ def tile_gcnlayer_kernel(tc, h, adj, W, b, bn_weight, bn_bias, res_weight, out):
         stage1_piece(1)
         for w in range(NT // 2):
             row_sums(w)
-            if w == 2:
-                dis_a(0)
-            if w == 3:
-                dis_b(0)
+            if w in (2, 4):
+                dis_group(w // 2 - 1)
             stage1_piece(2 + w)
             if w % 2 == 1:
                 diag_matmuls(w // 2)
@@ -366,23 +344,15 @@ def tile_gcnlayer_kernel(tc, h, adj, W, b, bn_weight, bn_bias, res_weight, out):
                 diag_copy(w // 2 - 1)
             if w == 2:
                 unit_transposes(0, 0)
-            if w == 3:
-                dis_c(0)
                 spread_matmuls(0)
+            if w == 3:
+                spread_copy(0)
         diag_copy(2)
-        spread_copy(0)
-        dis_a(1)
-        dis_a(2)
-        dis_b(1)
-        dis_b(2)
+        dis_group(2)
         unit_planes(0, 0)
         unit_transposes(0, 1)
-        stage1_piece(8)
-        dis_c(1)
-        dis_c(2)
-        stage1_piece(9)
-        stage1_piece(10)
-        stage1_piece(11)
+        for k in range(8, 12):
+            stage1_piece(k)
         spread_matmuls(1)
         spread_matmuls(2)
         held = None
@@ -400,11 +370,11 @@ def tile_gcnlayer_kernel(tc, h, adj, W, b, bn_weight, bn_bias, res_weight, out):
             unit_scale(c, g)
             if k >= 2 and units[k - 2][1] == NG - 1:
                 chunk_stats(units[k - 2][0])
+            if k + 2 <= last:
+                unit_transposes(*units[k + 2])
             if copied and held is not None:
                 unit_matmuls(*held)
                 held = None
-            if k + 2 <= last:
-                unit_transposes(*units[k + 2])
             if k >= 1:
                 if k < last:
                     unit_quant(*units[k - 1])
@@ -419,12 +389,10 @@ def tile_gcnlayer_kernel(tc, h, adj, W, b, bn_weight, bn_bias, res_weight, out):
         mv = const.tile([P, NJ, 2], F32, name="mv")
         for j in range(NJ):
             nc.vector.bn_aggr(out=mv[:, j, :], in_=st[:, j, :, :].rearrange("p c s -> p (c s)"))
-        ve = const.tile([P, NJ], F32, name="ve")
-        nc.vector.tensor_scalar(out=ve[:], in0=mv[:, :, 1], scalar1=BN_EPS, scalar2=None, op0=ALU.add)
-        sd = const.tile([P, NJ], F32, name="sd")
-        nc.scalar.activation(out=sd[:], in_=ve[:], func=ACT.Sqrt)
         rs = const.tile([P, NJ], F32, name="rs")
-        nc.vector.reciprocal(out=rs[:], in_=sd[:])
+        nc.scalar.activation(
+            out=rs[:], in_=mv[:, :, 1], func=ACT.Abs_reciprocal_sqrt, bias=epsb[:, 0:1]
+        )
         sc = const.tile([P, NJ], F32, name="sc")
         nc.vector.tensor_tensor(out=sc[:], in0=gb[:, 0:4], in1=rs[:], op=ALU.mult)
         ms = const.tile([P, NJ], F32, name="ms")

@@ -19,6 +19,7 @@ NG = NODES // 512
 NJ = FEAT // P
 BN_EPS = 1e-5
 PINNED = True
+VCOLS = 384
 
 FLOPS = 2 * NODES * FEAT * FEAT + 2 * NODES * NODES * FEAT
 
@@ -232,10 +233,7 @@ def tile_gcnlayer_kernel(tc, h, adj, W, b, bn_weight, bn_bias, res_weight, out):
         dps = {}
 
         def spread_matmuls(gq):
-            if gq == 0:
-                dp = ring.tile([P, 512], F32, name="dp", tag="ring")
-            else:
-                dp = ybank.tile([P, 512], F32, name="dpy%d" % gq, tag="y%d" % (gq - 1))
+            dp = ring.tile([P, 512], F32, name="dp", tag="ring")
             dps[gq] = dp
             for t in range(4):
                 nc.tensor.matmul(
@@ -247,37 +245,35 @@ def tile_gcnlayer_kernel(tc, h, adj, W, b, bn_weight, bn_bias, res_weight, out):
                 )
 
         def spread_copy(gq):
-            nc.scalar.copy(out=d_sb[:, 512 * gq : 512 * gq + 512], in_=dps[gq][:])
+            nc.scalar.copy(
+                out=d_sb[:, 512 * gq + VCOLS : 512 * gq + 512], in_=dps[gq][:, VCOLS:512]
+            )
 
         a_codes = keep.tile([P, NG, NODES], U32, name="a_codes", align_bytes=64)
         a_sc = keep.tile([P, NG, NODES], U8, name="a_sc", align_bytes=64)
         st = const.tile([P, NJ, NG, 6], F32, name="st")
         tus, fts, grps, ybs = {}, {}, {}, {}
 
-        def unit_transposes(c, g):
-            tus[(c, g)] = []
-            for u in range(2):
-                tu = ring.tile([P, 512], F32, name="tu", tag="ring")
-                for t in range(4):
-                    lo = 768 * (4 * c + t) + 128 * (2 * g + u)
-                    nc.tensor.transpose(
-                        tu[:, 128 * t : 128 * t + 128], a32[:, lo : lo + 128], ident_f[:]
-                    )
-                tus[(c, g)].append(tu)
-
-        def unit_planes(c, g):
-            f_t = fpool.tile([P, 4, 512], F32, name="f_t", tag="f_t")
-            fts[(c, g)] = f_t
+        def bank_transposes(c, g, u):
+            tu = ring.tile([P, 512], F32, name="tu", tag="ring")
             for t in range(4):
-                u, e = t // 2, t % 2
+                lo = 768 * (4 * c + t) + 128 * (2 * g + u)
+                nc.tensor.transpose(tu[:, 128 * t : 128 * t + 128], a32[:, lo : lo + 128], ident_f[:])
+            tus[(c, g, u)] = tu
+
+        def half_planes(c, g, u):
+            if u == 0:
+                fts[(c, g)] = fpool.tile([P, 4, 512], F32, name="f_t", tag="f_t")
+            f_t = fts[(c, g)]
+            for e in range(2):
+                t = 2 * u + e
                 nc.scalar.activation(
                     out=f_t[:, t, :],
-                    in_=tus[(c, g)][u][:].bitcast(BF16).rearrange("p (m e) -> p m e", e=2)[:, :, e],
+                    in_=tus[(c, g, u)][:].bitcast(BF16).rearrange("p (m e) -> p m e", e=2)[:, :, e],
                     func=ACT.Copy,
                     scale=dis[:, 4 * g + t : 4 * g + t + 1],
                 )
-            if c == g:
-                for t in range(4):
+                if c == g:
                     nc.scalar.activation(
                         out=f_t[:, t, 128 * t : 128 * t + 128],
                         in_=tmpd[:, 4 * g + t, :],
@@ -290,9 +286,17 @@ def tile_gcnlayer_kernel(tc, h, adj, W, b, bn_weight, bn_bias, res_weight, out):
             grp = gpool.tile([P, 2048], BF16, name="grp", tag="grp", align_bytes=64)
             grps[(c, g)] = grp
             nc.vector.tensor_tensor(
-                out=grp[:].rearrange("p (m t) -> p m t", t=4),
-                in0=fts[(c, g)][:].rearrange("p t m -> p m t"),
-                in1=d_sb[:, cs].unsqueeze(2).to_broadcast([P, 512, 4]),
+                out=grp[:, 0 : 4 * VCOLS].rearrange("p (m t) -> p m t", t=4),
+                in0=fts[(c, g)][:, :, 0:VCOLS].rearrange("p t m -> p m t"),
+                in1=dps[c][:, 0:VCOLS].unsqueeze(2).to_broadcast([P, VCOLS, 4]),
+                op=ALU.mult,
+            )
+            nc.gpsimd.tensor_tensor(
+                out=grp[:, 4 * VCOLS : 2048].rearrange("p (m t) -> p m t", t=4),
+                in0=fts[(c, g)][:, :, VCOLS:512].rearrange("p t m -> p m t"),
+                in1=d_sb[:, 512 * c + VCOLS : 512 * c + 512]
+                .unsqueeze(2)
+                .to_broadcast([P, 512 - VCOLS, 4]),
                 op=ALU.mult,
             )
 
@@ -331,6 +335,7 @@ def tile_gcnlayer_kernel(tc, h, adj, W, b, bn_weight, bn_bias, res_weight, out):
 
         units = [(c, g) for c in range(NG) for g in range(NG)]
         last = len(units) - 1
+        banks = [(c, g, u) for (c, g) in units for u in range(2)]
         stage1_piece(0)
         stage1_piece(1)
         for w in range(NT // 2):
@@ -343,25 +348,28 @@ def tile_gcnlayer_kernel(tc, h, adj, W, b, bn_weight, bn_bias, res_weight, out):
             if w % 2 == 0 and w > 0:
                 diag_copy(w // 2 - 1)
             if w == 2:
-                unit_transposes(0, 0)
+                bank_transposes(*banks[0])
+                bank_transposes(*banks[1])
                 spread_matmuls(0)
             if w == 3:
                 spread_copy(0)
         diag_copy(2)
         dis_group(2)
-        unit_planes(0, 0)
-        unit_transposes(0, 1)
+        bank_transposes(*banks[2])
+        issued = 3
         for k in range(8, 12):
             stage1_piece(k)
-        spread_matmuls(1)
-        spread_matmuls(2)
         held = None
         for k, (c, g) in enumerate(units):
-            if k > 0:
-                unit_planes(c, g)
-            if k == 1:
-                spread_copy(1)
-                spread_copy(2)
+            ahead = 2 if (g == NG - 1 and c + 1 < NG) else 3
+            for n in (2 * k, 2 * k + 1):
+                half_planes(*banks[n])
+                while issued < len(banks) and issued <= n + ahead:
+                    bank_transposes(*banks[issued])
+                    issued += 1
+            if g == NG - 1 and c + 1 < NG:
+                spread_matmuls(c + 1)
+                spread_copy(c + 1)
             copied = k >= 3 and units[k - 3][1] == NG - 1
             if copied:
                 chunk_copy(units[k - 3][0])
@@ -370,8 +378,6 @@ def tile_gcnlayer_kernel(tc, h, adj, W, b, bn_weight, bn_bias, res_weight, out):
             unit_scale(c, g)
             if k >= 2 and units[k - 2][1] == NG - 1:
                 chunk_stats(units[k - 2][0])
-            if k + 2 <= last:
-                unit_transposes(*units[k + 2])
             if copied and held is not None:
                 unit_matmuls(*held)
                 held = None

@@ -19,7 +19,6 @@ NG = NODES // 512
 NJ = FEAT // P
 BN_EPS = 1e-5
 PINNED = True
-VCOLS = 384
 
 FLOPS = 2 * NODES * FEAT * FEAT + 2 * NODES * NODES * FEAT
 
@@ -34,7 +33,7 @@ def tile_gcnlayer_kernel(tc, h, adj, W, b, bn_weight, bn_bias, res_weight, out):
         hlgp = ctx.enter_context(tc.tile_pool(name="hlgp", bufs=2))
         fpool = ctx.enter_context(tc.tile_pool(name="fpool", bufs=3))
         gpool = ctx.enter_context(tc.tile_pool(name="gpool", bufs=3))
-        opool = ctx.enter_context(tc.tile_pool(name="opool", bufs=4))
+        opool = ctx.enter_context(tc.tile_pool(name="opool", bufs=12))
         ring = ctx.enter_context(tc.psum_pool(name="ring", bufs=4))
         ybank = ctx.enter_context(tc.psum_pool(name="ybank", bufs=1))
 
@@ -233,7 +232,10 @@ def tile_gcnlayer_kernel(tc, h, adj, W, b, bn_weight, bn_bias, res_weight, out):
         dps = {}
 
         def spread_matmuls(gq):
-            dp = ring.tile([P, 512], F32, name="dp", tag="ring")
+            if gq == 0:
+                dp = ring.tile([P, 512], F32, name="dp", tag="ring")
+            else:
+                dp = ybank.tile([P, 512], F32, name="dpy%d" % gq, tag="y%d" % (gq - 1))
             dps[gq] = dp
             for t in range(4):
                 nc.tensor.matmul(
@@ -245,35 +247,37 @@ def tile_gcnlayer_kernel(tc, h, adj, W, b, bn_weight, bn_bias, res_weight, out):
                 )
 
         def spread_copy(gq):
-            nc.scalar.copy(
-                out=d_sb[:, 512 * gq + VCOLS : 512 * gq + 512], in_=dps[gq][:, VCOLS:512]
-            )
+            nc.scalar.copy(out=d_sb[:, 512 * gq : 512 * gq + 512], in_=dps[gq][:])
 
         a_codes = keep.tile([P, NG, NODES], U32, name="a_codes", align_bytes=64)
         a_sc = keep.tile([P, NG, NODES], U8, name="a_sc", align_bytes=64)
         st = const.tile([P, NJ, NG, 6], F32, name="st")
         tus, fts, grps, ybs = {}, {}, {}, {}
 
-        def bank_transposes(c, g, u):
-            tu = ring.tile([P, 512], F32, name="tu", tag="ring")
-            for t in range(4):
-                lo = 768 * (4 * c + t) + 128 * (2 * g + u)
-                nc.tensor.transpose(tu[:, 128 * t : 128 * t + 128], a32[:, lo : lo + 128], ident_f[:])
-            tus[(c, g, u)] = tu
+        def unit_transposes(c, g):
+            tus[(c, g)] = []
+            for u in range(2):
+                tu = ring.tile([P, 512], F32, name="tu", tag="ring")
+                for t in range(4):
+                    lo = 768 * (4 * c + t) + 128 * (2 * g + u)
+                    nc.tensor.transpose(
+                        tu[:, 128 * t : 128 * t + 128], a32[:, lo : lo + 128], ident_f[:]
+                    )
+                tus[(c, g)].append(tu)
 
-        def half_planes(c, g, u):
-            if u == 0:
-                fts[(c, g)] = fpool.tile([P, 4, 512], F32, name="f_t", tag="f_t")
-            f_t = fts[(c, g)]
-            for e in range(2):
-                t = 2 * u + e
+        def unit_planes(c, g):
+            f_t = fpool.tile([P, 4, 512], F32, name="f_t", tag="f_t")
+            fts[(c, g)] = f_t
+            for t in range(4):
+                u, e = t // 2, t % 2
                 nc.scalar.activation(
                     out=f_t[:, t, :],
-                    in_=tus[(c, g, u)][:].bitcast(BF16).rearrange("p (m e) -> p m e", e=2)[:, :, e],
+                    in_=tus[(c, g)][u][:].bitcast(BF16).rearrange("p (m e) -> p m e", e=2)[:, :, e],
                     func=ACT.Copy,
                     scale=dis[:, 4 * g + t : 4 * g + t + 1],
                 )
-                if c == g:
+            if c == g:
+                for t in range(4):
                     nc.scalar.activation(
                         out=f_t[:, t, 128 * t : 128 * t + 128],
                         in_=tmpd[:, 4 * g + t, :],
@@ -286,17 +290,9 @@ def tile_gcnlayer_kernel(tc, h, adj, W, b, bn_weight, bn_bias, res_weight, out):
             grp = gpool.tile([P, 2048], BF16, name="grp", tag="grp", align_bytes=64)
             grps[(c, g)] = grp
             nc.vector.tensor_tensor(
-                out=grp[:, 0 : 4 * VCOLS].rearrange("p (m t) -> p m t", t=4),
-                in0=fts[(c, g)][:, :, 0:VCOLS].rearrange("p t m -> p m t"),
-                in1=dps[c][:, 0:VCOLS].unsqueeze(2).to_broadcast([P, VCOLS, 4]),
-                op=ALU.mult,
-            )
-            nc.gpsimd.tensor_tensor(
-                out=grp[:, 4 * VCOLS : 2048].rearrange("p (m t) -> p m t", t=4),
-                in0=fts[(c, g)][:, :, VCOLS:512].rearrange("p t m -> p m t"),
-                in1=d_sb[:, 512 * c + VCOLS : 512 * c + 512]
-                .unsqueeze(2)
-                .to_broadcast([P, 512 - VCOLS, 4]),
+                out=grp[:].rearrange("p (m t) -> p m t", t=4),
+                in0=fts[(c, g)][:].rearrange("p t m -> p m t"),
+                in1=d_sb[:, cs].unsqueeze(2).to_broadcast([P, 512, 4]),
                 op=ALU.mult,
             )
 
@@ -335,7 +331,6 @@ def tile_gcnlayer_kernel(tc, h, adj, W, b, bn_weight, bn_bias, res_weight, out):
 
         units = [(c, g) for c in range(NG) for g in range(NG)]
         last = len(units) - 1
-        banks = [(c, g, u) for (c, g) in units for u in range(2)]
         stage1_piece(0)
         stage1_piece(1)
         for w in range(NT // 2):
@@ -348,28 +343,25 @@ def tile_gcnlayer_kernel(tc, h, adj, W, b, bn_weight, bn_bias, res_weight, out):
             if w % 2 == 0 and w > 0:
                 diag_copy(w // 2 - 1)
             if w == 2:
-                bank_transposes(*banks[0])
-                bank_transposes(*banks[1])
+                unit_transposes(0, 0)
                 spread_matmuls(0)
             if w == 3:
                 spread_copy(0)
         diag_copy(2)
         dis_group(2)
-        bank_transposes(*banks[2])
-        issued = 3
+        unit_planes(0, 0)
+        unit_transposes(0, 1)
         for k in range(8, 12):
             stage1_piece(k)
+        spread_matmuls(1)
+        spread_matmuls(2)
         held = None
         for k, (c, g) in enumerate(units):
-            ahead = 2 if (g == NG - 1 and c + 1 < NG) else 3
-            for n in (2 * k, 2 * k + 1):
-                half_planes(*banks[n])
-                while issued < len(banks) and issued <= n + ahead:
-                    bank_transposes(*banks[issued])
-                    issued += 1
-            if g == NG - 1 and c + 1 < NG:
-                spread_matmuls(c + 1)
-                spread_copy(c + 1)
+            if k > 0:
+                unit_planes(c, g)
+            if k == 1:
+                spread_copy(1)
+                spread_copy(2)
             copied = k >= 3 and units[k - 3][1] == NG - 1
             if copied:
                 chunk_copy(units[k - 3][0])
@@ -378,6 +370,8 @@ def tile_gcnlayer_kernel(tc, h, adj, W, b, bn_weight, bn_bias, res_weight, out):
             unit_scale(c, g)
             if k >= 2 and units[k - 2][1] == NG - 1:
                 chunk_stats(units[k - 2][0])
+            if k + 2 <= last:
+                unit_transposes(*units[k + 2])
             if copied and held is not None:
                 unit_matmuls(*held)
                 held = None

@@ -18,7 +18,8 @@ NT = NODES // P
 NG = NODES // 512
 NJ = FEAT // P
 BN_EPS = 1e-5
-PINNED = True
+VECTOR_ROW_SUMS = (1, 3, 5, 7)
+POOL_TILES = (3,)
 
 FLOPS = 2 * NODES * FEAT * FEAT + 2 * NODES * NODES * FEAT
 
@@ -26,20 +27,19 @@ FLOPS = 2 * NODES * FEAT * FEAT + 2 * NODES * NODES * FEAT
 def tile_gcnlayer_kernel(tc, h, adj, W, b, bn_weight, bn_bias, res_weight, out):
     nc = tc.nc
     with ExitStack() as ctx:
-        if PINNED:
-            ctx.enter_context(tc.manual_schedule())
         const = ctx.enter_context(tc.tile_pool(name="const", bufs=1))
         keep = ctx.enter_context(tc.tile_pool(name="keep", bufs=1))
         hlgp = ctx.enter_context(tc.tile_pool(name="hlgp", bufs=2))
-        fpool = ctx.enter_context(tc.tile_pool(name="fpool", bufs=3))
         gpool = ctx.enter_context(tc.tile_pool(name="gpool", bufs=3))
-        opool = ctx.enter_context(tc.tile_pool(name="opool", bufs=12))
-        ring = ctx.enter_context(tc.psum_pool(name="ring", bufs=4))
-        ybank = ctx.enter_context(tc.psum_pool(name="ybank", bufs=1))
+        xpool = ctx.enter_context(tc.tile_pool(name="xpool", bufs=2))
+        opool = ctx.enter_context(tc.tile_pool(name="opool", bufs=6))
+        ring = ctx.enter_context(tc.psum_pool(name="ring", bufs=3))
+        ypool = ctx.enter_context(tc.psum_pool(name="ypool", bufs=2))
+        dpool = ctx.enter_context(tc.psum_pool(name="dpool", bufs=1))
 
-        h_v = h.rearrange("o (w q e) k -> q (o w) e k", q=P, e=2)
-        adj_v = adj.rearrange("o (w q e) n -> q (o w) e n", q=P, e=2)
-        out_v = out.rearrange("o (w q e) f -> q (o w) e f", q=P, e=2)
+        h_v = h.rearrange("o (t q) k -> q (o t) k", q=P)
+        adj_v = adj.rearrange("o (t q) n -> q (o t) n", q=P)
+        out_v = out.rearrange("o (t q) f -> q (o t) f", q=P)
 
         w_sb = keep.tile([P, NJ * FEAT], BF16, name="w_sb")
         nc.sync.dma_start(
@@ -49,16 +49,15 @@ def tile_gcnlayer_kernel(tc, h, adj, W, b, bn_weight, bn_bias, res_weight, out):
         h_sb = keep.tile([P, NT * FEAT], BF16, name="h_sb")
         for g in range(NG):
             nc.sync.dma_start(
-                out=h_sb[:, 2048 * g : 2048 * g + 2048].rearrange("q (w x) -> q w x", w=2),
-                in_=h_v[:, 2 * g : 2 * g + 2, :, :].rearrange("q w e k -> q w (e k)"),
+                out=h_sb[:, 2048 * g : 2048 * g + 2048].rearrange("q (t k) -> q t k", t=4),
+                in_=h_v[:, 4 * g : 4 * g + 4, :],
             )
         a_sb = keep.tile([P, NT * NODES], BF16, name="a_sb")
         for w in range(NT // 2):
             nc.sync.dma_start(
-                out=a_sb[:, 2 * NODES * w : 2 * NODES * (w + 1)],
-                in_=adj_v[:, w, :, :].rearrange("q e n -> q (e n)"),
+                out=a_sb[:, 2 * NODES * w : 2 * NODES * (w + 1)].rearrange("q (t n) -> q t n", t=2),
+                in_=adj_v[:, 2 * w : 2 * w + 2, :],
             )
-        a32 = a_sb[:].bitcast(F32)
 
         ident_f = const.tile([P, P], F32, name="ident_f")
         make_identity(nc, ident_f[:])
@@ -79,8 +78,6 @@ def tile_gcnlayer_kernel(tc, h, adj, W, b, bn_weight, bn_bias, res_weight, out):
         nc.vector.memset(one1[:], 1.0)
         junk = const.tile([P, 1], F32, name="junk")
         nc.scalar.activation(out=junk[:], in_=one1[:], func=ACT.Abs_reciprocal_sqrt)
-        epsb = const.tile([P, 1], F32, name="epsb")
-        nc.vector.memset(epsb[:], BN_EPS)
 
         b_bc = const.tile([P, FEAT], BF16, name="b_bc")
         gb = const.tile([P, 8], F32, name="gb")
@@ -95,22 +92,28 @@ def tile_gcnlayer_kernel(tc, h, adj, W, b, bn_weight, bn_bias, res_weight, out):
             nc.vector.tensor_copy(out=gb[:], in_=vt_ps[:, 0:8])
             nc.vector.tensor_copy(out=res_f[:], in_=res_b[:])
 
-        def words_to_k(src32, pair, grouped32):
+        def words_to_k(src32, pair, grouped32, eng, split_rows):
             xt = ring.tile([P, 512], F32, name="xt", tag="ring")
             for r2 in range(2):
                 for u in range(2):
                     lo = 256 * (2 * pair + r2) + 128 * u
                     nc.tensor.transpose(
-                        xt[:, 256 * r2 + 128 * u : 256 * r2 + 128 * u + 128],
+                        xt[:, 256 * u + 128 * r2 : 256 * u + 128 * r2 + 128],
                         src32[:, lo : lo + 128],
                         ident_f[:],
                     )
-            nc.scalar.copy(
-                out=grouped32[:, 512 * pair : 512 * pair + 512].rearrange(
-                    "p (r q u) -> p r q u", r=2, u=2
-                ),
-                in_=xt[:].rearrange("p (r u q) -> p r q u", r=2, u=2),
-            )
+            copy = nc.scalar.copy if eng == "S" else nc.vector.tensor_copy
+            dst = grouped32[:, 512 * pair : 512 * pair + 512]
+            if split_rows:
+                copy(
+                    out=dst.rearrange("p (e q u) -> p e q u", e=2, u=2),
+                    in_=xt[:].rearrange("p (u q e) -> p e q u", u=2, e=2),
+                )
+            else:
+                copy(
+                    out=dst.rearrange("p (r u) -> p r u", u=2),
+                    in_=xt[:].rearrange("p (u r) -> p r u", u=2),
+                )
 
         wg = keep.tile([P, 4 * FEAT], BF16, name="wg", align_bytes=64)
         w_codes = keep.tile([P, FEAT], U32, name="w_codes", align_bytes=64)
@@ -118,19 +121,20 @@ def tile_gcnlayer_kernel(tc, h, adj, W, b, bn_weight, bn_bias, res_weight, out):
         hg = keep.tile([P, 4 * NODES], BF16, name="hg", align_bytes=64)
         h_codes = keep.tile([P, NODES], U32, name="h_codes", align_bytes=64)
         h_sc = keep.tile([P, NODES], U8, name="h_sc", align_bytes=64)
-        for pair in range(2):
-            words_to_k(w_sb[:].bitcast(F32), pair, wg[:].bitcast(F32))
-        nc.vector.quantize_mx(out=w_codes[:].bitcast(FP8X4), scales=w_sc[:], in_=wg[:])
-        for g in range(NG):
+
+        def stage0_w():
+            for pair in range(2):
+                words_to_k(w_sb[:].bitcast(F32), pair, wg[:].bitcast(F32), "SV"[pair], False)
+            nc.vector.quantize_mx(out=w_codes[:].bitcast(FP8X4), scales=w_sc[:], in_=wg[:])
+
+        def stage0_h(g):
             for pair in (2 * g, 2 * g + 1):
-                words_to_k(h_sb[:].bitcast(F32), pair, hg[:].bitcast(F32))
+                words_to_k(h_sb[:].bitcast(F32), pair, hg[:].bitcast(F32), "SS"[pair % 2], True)
             nc.vector.quantize_mx(
                 out=h_codes[:, 512 * g : 512 * g + 512].bitcast(FP8X4),
                 scales=h_sc[:, 512 * g : 512 * g + 512],
                 in_=hg[:, 2048 * g : 2048 * g + 2048],
             )
-            if g == 0:
-                small_vectors()
 
         hl_codes = keep.tile([P, NG * FEAT], U32, name="hl_codes", align_bytes=64)
         hl_sc = keep.tile([P, NG * FEAT], U8, name="hl_sc", align_bytes=64)
@@ -140,7 +144,7 @@ def tile_gcnlayer_kernel(tc, h, adj, W, b, bn_weight, bn_bias, res_weight, out):
             g, fc = k // NJ, k % NJ
             if fc == 0:
                 hlgs[g] = hlgp.tile([P, 4 * FEAT], BF16, name="hlg", tag="hlg", align_bytes=64)
-            yb = ybank.tile([P, 512], F32, name="y%d" % fc, tag="y%d" % fc)
+            yb = ypool.tile([P, 512], F32, name="yb", tag="y")
             for t in range(4):
                 i = 4 * g + t
                 nc.tensor.matmul_mx(
@@ -168,132 +172,132 @@ def tile_gcnlayer_kernel(tc, h, adj, W, b, bn_weight, bn_bias, res_weight, out):
         zs = keep.tile([P, NJ, NODES], F32, name="zs")
         junk_s = zs[:, 0, 0 : NODES // 2].bitcast(BF16)
         junk_v = zs[:, 1, 0 : NODES // 2].bitcast(BF16)
-        deg_s = const.tile([P, NT // 2], F32, name="deg_s")
-        deg_v = const.tile([P, NT // 2], F32, name="deg_v")
+        deg = const.tile([P, NT], F32, name="deg")
         dis = const.tile([P, NT], F32, name="dis")
         d_sb = keep.tile([P, NODES], F32, name="d_sb")
-        tmpd = keep.tile([P, NT, P], F32, name="tmpd")
+        adj_i = keep.tile([P, NT, P], F32, name="adj_i")
 
-        def row_sums(w):
-            nc.scalar.activation(
-                out=junk_s,
-                in_=a_sb[:, NODES * 2 * w : NODES * (2 * w + 1)],
-                func=ACT.Copy,
-                accum_out=deg_s[:, w : w + 1],
-            )
-            nc.vector.tensor_scalar(
-                out=junk_v,
-                in0=a_sb[:, NODES * (2 * w + 1) : NODES * (2 * w + 2)],
-                scalar1=1.0,
-                scalar2=None,
-                op0=ALU.mult,
-                op1=ALU.add,
-                accum_out=deg_v[:, w : w + 1],
-            )
-
-        def dis_group(gq):
-            dv = dis[:, 4 * gq : 4 * gq + 4].rearrange("p (w e) -> p w e", e=2)
-            for e, deg in ((0, deg_s), (1, deg_v)):
+        def row_sum(i):
+            if i in VECTOR_ROW_SUMS:
+                nc.vector.tensor_scalar(
+                    out=junk_v,
+                    in0=a_sb[:, NODES * i : NODES * (i + 1)],
+                    scalar1=1.0,
+                    scalar2=None,
+                    op0=ALU.mult,
+                    op1=ALU.add,
+                    accum_out=deg[:, i : i + 1],
+                )
+            else:
                 nc.scalar.activation(
-                    out=dv[:, :, e],
-                    in_=deg[:, 2 * gq : 2 * gq + 2],
-                    func=ACT.Abs_reciprocal_sqrt,
-                    bias=one1[:, 0:1],
+                    out=junk_s,
+                    in_=a_sb[:, NODES * i : NODES * (i + 1)],
+                    func=ACT.Copy,
+                    accum_out=deg[:, i : i + 1],
                 )
 
-        dgs = {}
+        def diag_block(i):
+            lo = NODES * i + P * i
+            nc.gpsimd.tensor_tensor(
+                out=adj_i[:, i, :], in0=a_sb[:, lo : lo + P], in1=ident_f[:], op=ALU.add
+            )
 
-        def diag_matmuls(c):
-            dg = ring.tile([P, 512], F32, name="dg", tag="ring")
-            dgs[c] = dg
-            for t in range(4):
-                i = 4 * c + t
-                lo = NODES * i + 256 * (i // 2)
-                nc.tensor.matmul(
-                    out=dg[:, 128 * t : 128 * t + 128],
-                    lhsT=a_sb[:, lo : lo + 256].rearrange("q (p e) -> q p e", e=2)[:, :, i % 2],
-                    rhs=ident_b[:],
-                    start=True,
-                    stop=False,
-                )
-                nc.tensor.matmul(
-                    out=dg[:, 128 * t : 128 * t + 128],
-                    lhsT=ident_b[:],
-                    rhs=ident_b[:],
-                    start=False,
-                    stop=True,
-                )
-
-        def diag_copy(c):
-            nc.scalar.copy(
-                out=tmpd[:, 4 * c : 4 * c + 4, :].rearrange("p t x -> p (t x)"), in_=dgs[c][:]
+        def dis_group(c):
+            nc.scalar.activation(
+                out=dis[:, 4 * c : 4 * c + 4],
+                in_=deg[:, 4 * c : 4 * c + 4],
+                func=ACT.Abs_reciprocal_sqrt,
+                bias=one1[:, 0:1],
             )
 
         dps = {}
 
-        def spread_matmuls(gq):
-            if gq == 0:
-                dp = ring.tile([P, 512], F32, name="dp", tag="ring")
-            else:
-                dp = ybank.tile([P, 512], F32, name="dpy%d" % gq, tag="y%d" % (gq - 1))
-            dps[gq] = dp
+        def spread_matmuls(c):
+            dp = dpool.tile([P, 512], F32, name="dp%d" % c, tag="d%d" % c)
+            dps[c] = dp
             for t in range(4):
                 nc.tensor.matmul(
                     out=dp[:, 128 * t : 128 * t + 128],
-                    lhsT=dis[:, 4 * gq + t : 4 * gq + t + 1].to_broadcast([P, P]),
+                    lhsT=dis[:, 4 * c + t : 4 * c + t + 1].to_broadcast([P, P]),
                     rhs=ident_f[:],
                     start=True,
                     stop=True,
                 )
 
-        def spread_copy(gq):
-            nc.scalar.copy(out=d_sb[:, 512 * gq : 512 * gq + 512], in_=dps[gq][:])
+        def spread_copy(c):
+            nc.scalar.copy(out=d_sb[:, 512 * c : 512 * c + 512], in_=dps[c][:])
 
+        ah = keep.tile([P, NT * NODES], BF16, name="ah")
+        ah32 = ah[:].bitcast(F32)
         a_codes = keep.tile([P, NG, NODES], U32, name="a_codes", align_bytes=64)
         a_sc = keep.tile([P, NG, NODES], U8, name="a_sc", align_bytes=64)
         st = const.tile([P, NJ, NG, 6], F32, name="st")
-        tus, fts, grps, ybs = {}, {}, {}, {}
+        tus, grps, ybs = {}, {}, {}
 
-        def unit_transposes(c, g):
-            tus[(c, g)] = []
-            for u in range(2):
-                tu = ring.tile([P, 512], F32, name="tu", tag="ring")
-                for t in range(4):
-                    lo = 768 * (4 * c + t) + 128 * (2 * g + u)
-                    nc.tensor.transpose(
-                        tu[:, 128 * t : 128 * t + 128], a32[:, lo : lo + 128], ident_f[:]
-                    )
-                tus[(c, g)].append(tu)
-
-        def unit_planes(c, g):
-            f_t = fpool.tile([P, 4, 512], F32, name="f_t", tag="f_t")
-            fts[(c, g)] = f_t
-            for t in range(4):
-                u, e = t // 2, t % 2
-                nc.scalar.activation(
-                    out=f_t[:, t, :],
-                    in_=tus[(c, g)][u][:].bitcast(BF16).rearrange("p (m e) -> p m e", e=2)[:, :, e],
-                    func=ACT.Copy,
-                    scale=dis[:, 4 * g + t : 4 * g + t + 1],
+        def scale_on_vector(i, g):
+            lo = NODES * i + 512 * g
+            nc.vector.scalar_tensor_tensor(
+                out=ah[:, lo : lo + 512],
+                in0=a_sb[:, lo : lo + 512],
+                scalar=dis[:, i : i + 1],
+                in1=dps[g][:],
+                op0=ALU.mult,
+                op1=ALU.mult,
+            )
+            if i // 4 == g:
+                lo = NODES * i + P * i
+                nc.vector.scalar_tensor_tensor(
+                    out=ah[:, lo : lo + P],
+                    in0=adj_i[:, i, :],
+                    scalar=dis[:, i : i + 1],
+                    in1=dps[g][:, P * (i % 4) : P * (i % 4) + P],
+                    op0=ALU.mult,
+                    op1=ALU.mult,
                 )
-            if c == g:
-                for t in range(4):
-                    nc.scalar.activation(
-                        out=f_t[:, t, 128 * t : 128 * t + 128],
-                        in_=tmpd[:, 4 * g + t, :],
-                        func=ACT.Copy,
-                        scale=dis[:, 4 * g + t : 4 * g + t + 1],
+
+        def scale_on_pool(i, g):
+            lo = NODES * i + 512 * g
+            xs = xpool.tile([P, 512], F32, name="xs", tag="xs")
+            nc.gpsimd.tensor_scalar(
+                out=xs[:], in0=a_sb[:, lo : lo + 512], scalar1=dis[:, i : i + 1], scalar2=1.0,
+                op0=ALU.mult, op1=ALU.mult,
+            )
+            if i // 4 == g:
+                nc.gpsimd.tensor_scalar(
+                    out=xs[:, P * (i % 4) : P * (i % 4) + P], in0=adj_i[:, i, :], scalar1=dis[:, i : i + 1],
+                    scalar2=1.0, op0=ALU.mult, op1=ALU.mult,
+                )
+            nc.gpsimd.tensor_tensor(
+                out=ah[:, lo : lo + 512], in0=xs[:], in1=d_sb[:, 512 * g : 512 * g + 512], op=ALU.mult
+            )
+
+        def unit_scale(c, g, half):
+            for t in (2 * half, 2 * half + 1):
+                if t in POOL_TILES:
+                    scale_on_pool(4 * c + t, g)
+                else:
+                    scale_on_vector(4 * c + t, g)
+
+        def unit_transposes(c, g, half):
+            tu = ring.tile([P, 512], F32, name="tu", tag="ring")
+            tus[(c, g, half)] = tu
+            for u in range(2):
+                for e2 in range(2):
+                    lo = 768 * (4 * c + 2 * half + e2) + 256 * g + 128 * u
+                    nc.tensor.transpose(
+                        tu[:, 256 * u + 128 * e2 : 256 * u + 128 * e2 + 128],
+                        ah32[:, lo : lo + 128],
+                        ident_f[:],
                     )
 
-        def unit_scale(c, g):
-            cs = slice(512 * c, 512 * c + 512)
-            grp = gpool.tile([P, 2048], BF16, name="grp", tag="grp", align_bytes=64)
-            grps[(c, g)] = grp
-            nc.vector.tensor_tensor(
-                out=grp[:].rearrange("p (m t) -> p m t", t=4),
-                in0=fts[(c, g)][:].rearrange("p t m -> p m t"),
-                in1=d_sb[:, cs].unsqueeze(2).to_broadcast([P, 512, 4]),
-                op=ALU.mult,
+        def unit_words(c, g, half):
+            if half == 0:
+                grps[(c, g)] = gpool.tile([P, 2048], BF16, name="grp", tag="grp", align_bytes=64)
+            nc.scalar.copy(
+                out=grps[(c, g)][:].bitcast(F32)[:, 512 * half : 512 * half + 512].rearrange(
+                    "p (m u) -> p m u", u=2
+                ),
+                in_=tus[(c, g, half)][:].rearrange("p (u m) -> p m u", u=2),
             )
 
         def unit_quant(c, g):
@@ -302,97 +306,113 @@ def tile_gcnlayer_kernel(tc, h, adj, W, b, bn_weight, bn_bias, res_weight, out):
                 out=a_codes[:, g, cs].bitcast(FP8X4), scales=a_sc[:, g, cs], in_=grps[(c, g)][:]
             )
 
-        def unit_matmuls(c, g):
+        def one_pass(yb, c, g, j):
             cs = slice(512 * c, 512 * c + 512)
-            if g == 0:
-                ybs[c] = [
-                    ybank.tile([P, 512], F32, name="y%d" % j, tag="y%d" % j) for j in range(NJ)
-                ]
+            lo = 512 * g + 128 * j
+            nc.tensor.matmul_mx(
+                out=yb[:],
+                lhsT=hl_codes[:, lo : lo + 128].bitcast(FP8X4),
+                lhsT_scale=hl_sc[:, lo : lo + 128],
+                rhs=a_codes[:, g, cs].bitcast(FP8X4),
+                rhs_scale=a_sc[:, g, cs],
+                start=(g == 0),
+                stop=(g == NG - 1),
+            )
+
+        def chunk_matmuls(c):
+            cs = slice(512 * c, 512 * c + 512)
             for j in range(NJ):
-                lo = 512 * g + 128 * j
-                nc.tensor.matmul_mx(
-                    out=ybs[c][j][:],
-                    lhsT=hl_codes[:, lo : lo + 128].bitcast(FP8X4),
-                    lhsT_scale=hl_sc[:, lo : lo + 128],
-                    rhs=a_codes[:, g, cs].bitcast(FP8X4),
-                    rhs_scale=a_sc[:, g, cs],
-                    start=(g == 0),
-                    stop=(g == NG - 1),
-                )
+                yb = ypool.tile([P, 512], F32, name="yb", tag="y")
+                for g in range(NG):
+                    one_pass(yb, c, g, j)
+                nc.scalar.copy(out=zs[:, j, cs], in_=yb[:])
 
         def chunk_stats(c):
-            for j in range(NJ):
-                nc.vector.bn_stats(out=st[:, j, c, :], in_=ybs[c][j][:])
-
-        def chunk_copy(c):
             cs = slice(512 * c, 512 * c + 512)
             for j in range(NJ):
-                nc.scalar.copy(out=zs[:, j, cs], in_=ybs[c][j][:])
+                nc.vector.bn_stats(out=st[:, j, c, :], in_=(zs[:, j, cs] if c < NG - 1 else ybs[j][:]))
 
-        units = [(c, g) for c in range(NG) for g in range(NG)]
-        last = len(units) - 1
-        stage1_piece(0)
-        stage1_piece(1)
-        for w in range(NT // 2):
-            row_sums(w)
-            if w in (2, 4):
-                dis_group(w // 2 - 1)
-            stage1_piece(2 + w)
-            if w % 2 == 1:
-                diag_matmuls(w // 2)
-            if w % 2 == 0 and w > 0:
-                diag_copy(w // 2 - 1)
-            if w == 2:
-                unit_transposes(0, 0)
-                spread_matmuls(0)
-            if w == 3:
-                spread_copy(0)
-        diag_copy(2)
-        dis_group(2)
-        unit_planes(0, 0)
-        unit_transposes(0, 1)
-        for k in range(8, 12):
+        def last_chunk_banks():
+            ybs[0] = ypool.tile([P, 512], F32, name="yb", tag="y")
+            ybs[1] = ypool.tile([P, 512], F32, name="yb", tag="y")
+            ybs[2] = dpool.tile([P, 512], F32, name="yd0", tag="d0")
+            ybs[3] = dpool.tile([P, 512], F32, name="yd1", tag="d1")
+
+        def last_chunk_matmuls(g):
+            for j in range(NJ):
+                one_pass(ybs[j], NG - 1, g, j)
+
+        def front(c, g):
+            for half in range(2):
+                unit_scale(c, g, half)
+                unit_transposes(c, g, half)
+                unit_words(c, g, half)
+
+        stage0_w()
+        stage0_h(0)
+        small_vectors()
+        stage0_h(1)
+        for k in range(4):
             stage1_piece(k)
+        stage0_h(2)
+        for i in range(4):
+            row_sum(i)
+            diag_block(i)
+            stage1_piece(4 + i)
+        dis_group(0)
+        spread_matmuls(0)
+        spread_copy(0)
+        for i in range(4, 8):
+            row_sum(i)
+            diag_block(i)
+            stage1_piece(4 + i)
+        dis_group(1)
         spread_matmuls(1)
+        spread_copy(1)
+        front(0, 0)
+        row_sum(8)
+        diag_block(8)
+        row_sum(9)
+        diag_block(9)
+        front(0, 1)
+        unit_quant(0, 0)
+        row_sum(10)
+        diag_block(10)
+        row_sum(11)
+        diag_block(11)
+        dis_group(2)
         spread_matmuls(2)
-        held = None
-        for k, (c, g) in enumerate(units):
-            if k > 0:
-                unit_planes(c, g)
-            if k == 1:
-                spread_copy(1)
-                spread_copy(2)
-            copied = k >= 3 and units[k - 3][1] == NG - 1
-            if copied:
-                chunk_copy(units[k - 3][0])
-            if k == last:
-                unit_quant(*units[k - 1])
-            unit_scale(c, g)
-            if k >= 2 and units[k - 2][1] == NG - 1:
-                chunk_stats(units[k - 2][0])
-            if k + 2 <= last:
-                unit_transposes(*units[k + 2])
-            if copied and held is not None:
-                unit_matmuls(*held)
-                held = None
-            if k >= 1:
-                if k < last:
-                    unit_quant(*units[k - 1])
-                if units[k - 1][1] == 0 and units[k - 1][0] > 0:
-                    held = units[k - 1]
-                else:
-                    unit_matmuls(*units[k - 1])
-        unit_quant(*units[last])
-        unit_matmuls(*units[last])
-        chunk_stats(NG - 1)
+        spread_copy(2)
+        front(1, 0)
+        unit_quant(0, 1)
+        front(1, 1)
+        unit_quant(1, 0)
+        front(0, 2)
+        unit_quant(1, 1)
+        front(1, 2)
+        unit_quant(0, 2)
+        chunk_matmuls(0)
+        front(2, 0)
+        unit_quant(1, 2)
+        chunk_matmuls(1)
+        chunk_stats(0)
+        front(2, 1)
+        unit_quant(2, 0)
+        front(2, 2)
+        chunk_stats(1)
+        last_chunk_banks()
+        last_chunk_matmuls(0)
+        unit_quant(2, 1)
+        last_chunk_matmuls(1)
+        unit_quant(2, 2)
+        last_chunk_matmuls(2)
+        chunk_stats(2)
 
         mv = const.tile([P, NJ, 2], F32, name="mv")
         for j in range(NJ):
             nc.vector.bn_aggr(out=mv[:, j, :], in_=st[:, j, :, :].rearrange("p c s -> p (c s)"))
         rs = const.tile([P, NJ], F32, name="rs")
-        nc.scalar.activation(
-            out=rs[:], in_=mv[:, :, 1], func=ACT.Abs_reciprocal_sqrt, bias=epsb[:, 0:1]
-        )
+        nc.scalar.activation(out=rs[:], in_=mv[:, :, 1], func=ACT.Abs_reciprocal_sqrt, bias=BN_EPS)
         sc = const.tile([P, NJ], F32, name="sc")
         nc.vector.tensor_tensor(out=sc[:], in0=gb[:, 0:4], in1=rs[:], op=ALU.mult)
         ms = const.tile([P, NJ], F32, name="ms")
@@ -405,7 +425,7 @@ def tile_gcnlayer_kernel(tc, h, adj, W, b, bn_weight, bn_bias, res_weight, out):
             if eng == "S":
                 nc.scalar.activation(
                     out=zs[:, j, cs],
-                    in_=(zs[:, j, cs] if c < NG - 1 else ybs[c][j][:]),
+                    in_=(zs[:, j, cs] if c < NG - 1 else ybs[j][:]),
                     func=ACT.Relu,
                     scale=sc[:, j : j + 1],
                     bias=sh[:, j : j + 1],
@@ -446,4 +466,4 @@ def tile_gcnlayer_kernel(tc, h, adj, W, b, bn_weight, bn_bias, res_weight, out):
                 op0=ALU.mult,
                 op1=ALU.add,
             )
-            nc.sync.dma_start(out=out_v[:, i // 2, i % 2, :], in_=o_sb[:])
+            nc.sync.dma_start(out=out_v[:, i, :], in_=o_sb[:])

@@ -18,8 +18,11 @@ NT = NODES // P
 NG = NODES // 512
 NJ = FEAT // P
 BN_EPS = 1e-5
-VECTOR_ROW_SUMS = (1, 3, 5, 7)
+VECTOR_ROW_SUMS = (0, 1, 3, 4, 5, 7, 8, 9, 11)
 POOL_TILES = (3,)
+SCALAR_STATS = (0,)
+NORMALISE_PIECES = ((0, 128), (128, 512), (512, 1024), (1024, 1536))
+VECTOR_WORDS = ()
 
 FLOPS = 2 * NODES * FEAT * FEAT + 2 * NODES * NODES * FEAT
 
@@ -27,12 +30,13 @@ FLOPS = 2 * NODES * FEAT * FEAT + 2 * NODES * NODES * FEAT
 def tile_gcnlayer_kernel(tc, h, adj, W, b, bn_weight, bn_bias, res_weight, out):
     nc = tc.nc
     with ExitStack() as ctx:
+        ctx.enter_context(tc.manual_schedule(engines={mybir.EngineType.Pool}))
         const = ctx.enter_context(tc.tile_pool(name="const", bufs=1))
         keep = ctx.enter_context(tc.tile_pool(name="keep", bufs=1))
         hlgp = ctx.enter_context(tc.tile_pool(name="hlgp", bufs=2))
         gpool = ctx.enter_context(tc.tile_pool(name="gpool", bufs=3))
         xpool = ctx.enter_context(tc.tile_pool(name="xpool", bufs=2))
-        opool = ctx.enter_context(tc.tile_pool(name="opool", bufs=6))
+        opool = ctx.enter_context(tc.tile_pool(name="opool", bufs=12))
         ring = ctx.enter_context(tc.psum_pool(name="ring", bufs=3))
         ypool = ctx.enter_context(tc.psum_pool(name="ypool", bufs=2))
         dpool = ctx.enter_context(tc.psum_pool(name="dpool", bufs=1))
@@ -65,32 +69,29 @@ def tile_gcnlayer_kernel(tc, h, adj, W, b, bn_weight, bn_bias, res_weight, out):
         make_identity(nc, ident_b[:])
         ones = const.tile([P, P], BF16, name="ones")
         nc.vector.memset(ones[:], 1.0)
-        zb = const.tile([P, FEAT], BF16, name="zb")
-        nc.vector.memset(zb[:], 0.0)
         vt = const.tile([P, P], BF16, name="vt")
         nc.vector.memset(vt[:], 0.0)
-        nc.scalar.dma_start(out=zb[0:1, :], in_=b.rearrange("(o f) -> o f", o=1))
         nc.scalar.dma_start(out=vt[0:4, :], in_=bn_weight.rearrange("(j p) -> j p", p=P))
         nc.scalar.dma_start(out=vt[4:8, :], in_=bn_bias.rearrange("(j p) -> j p", p=P))
-        res_b = const.tile([P, 1], BF16, name="res_b")
-        nc.scalar.dma_start(out=res_b[:], in_=res_weight.partition_broadcast(P))
+        nc.scalar.dma_start(out=vt[8:12, :], in_=b.rearrange("(j p) -> j p", p=P))
+        zr = const.tile([P, 2], BF16, name="zr")
+        nc.vector.memset(zr[:], 0.0)
+        nc.scalar.dma_start(out=zr[0:1, 0:1], in_=res_weight.rearrange("(o f) -> o f", o=1))
         one1 = const.tile([P, 1], F32, name="one1")
         nc.vector.memset(one1[:], 1.0)
         junk = const.tile([P, 1], F32, name="junk")
         nc.scalar.activation(out=junk[:], in_=one1[:], func=ACT.Abs_reciprocal_sqrt)
 
-        b_bc = const.tile([P, FEAT], BF16, name="b_bc")
-        gb = const.tile([P, 8], F32, name="gb")
+        gb = const.tile([P, 12], F32, name="gb")
         res_f = const.tile([P, 1], F32, name="res_f")
 
         def small_vectors():
-            bb_ps = ring.tile([P, FEAT], F32, name="bb_ps", tag="ring")
-            nc.tensor.matmul(out=bb_ps[:], lhsT=ones[:], rhs=zb[:], start=True, stop=True)
-            nc.scalar.copy(out=b_bc[:], in_=bb_ps[:])
             vt_ps = ring.tile([P, P], BF16, name="vt_ps", tag="ring")
             nc.tensor.transpose(vt_ps[:], vt[:], ident_b[:])
-            nc.vector.tensor_copy(out=gb[:], in_=vt_ps[:, 0:8])
-            nc.vector.tensor_copy(out=res_f[:], in_=res_b[:])
+            nc.vector.tensor_copy(out=gb[:], in_=vt_ps[:, 0:12])
+            rp = ring.tile([P, 2], F32, name="rp", tag="ring")
+            nc.tensor.matmul(out=rp[:], lhsT=ones[:], rhs=zr[:], start=True, stop=True)
+            nc.vector.tensor_copy(out=res_f[:], in_=rp[:, 0:1])
 
         def words_to_k(src32, pair, grouped32, eng, split_rows):
             xt = ring.tile([P, 512], F32, name="xt", tag="ring")
@@ -129,7 +130,9 @@ def tile_gcnlayer_kernel(tc, h, adj, W, b, bn_weight, bn_bias, res_weight, out):
 
         def stage0_h(g):
             for pair in (2 * g, 2 * g + 1):
-                words_to_k(h_sb[:].bitcast(F32), pair, hg[:].bitcast(F32), "SS"[pair % 2], True)
+                words_to_k(h_sb[:].bitcast(F32), pair, hg[:].bitcast(F32), "S", False)
+
+        def stage0_hq(g):
             nc.vector.quantize_mx(
                 out=h_codes[:, 512 * g : 512 * g + 512].bitcast(FP8X4),
                 scales=h_sc[:, 512 * g : 512 * g + 512],
@@ -140,34 +143,56 @@ def tile_gcnlayer_kernel(tc, h, adj, W, b, bn_weight, bn_bias, res_weight, out):
         hl_sc = keep.tile([P, NG * FEAT], U8, name="hl_sc", align_bytes=64)
         hlgs = {}
 
-        def stage1_piece(k):
-            g, fc = k // NJ, k % NJ
-            if fc == 0:
-                hlgs[g] = hlgp.tile([P, 4 * FEAT], BF16, name="hlg", tag="hlg", align_bytes=64)
-            yb = ypool.tile([P, 512], F32, name="yb", tag="y")
-            for t in range(4):
-                i = 4 * g + t
-                nc.tensor.matmul_mx(
-                    out=yb[:, 128 * t : 128 * t + 128],
-                    lhsT=h_codes[:, 128 * i : 128 * i + 128].bitcast(FP8X4),
-                    lhsT_scale=h_sc[:, 128 * i : 128 * i + 128],
-                    rhs=w_codes[:, 128 * fc : 128 * fc + 128].bitcast(FP8X4),
-                    rhs_scale=w_sc[:, 128 * fc : 128 * fc + 128],
-                    start=True,
-                    stop=True,
-                )
-            nc.vector.tensor_tensor(
-                out=hlgs[g][:, 512 * fc : 512 * fc + 512].rearrange("p (f t) -> p f t", t=4),
-                in0=yb[:].rearrange("p (t f) -> p f t", t=4),
-                in1=b_bc[:, 128 * fc : 128 * fc + 128].unsqueeze(2).to_broadcast([P, 128, 4]),
-                op=ALU.add,
-            )
-            if fc == NJ - 1:
+        s1b = {}
+
+        def stage1_quant(g):
+            if True:
                 nc.vector.quantize_mx(
                     out=hl_codes[:, 512 * g : 512 * g + 512].bitcast(FP8X4),
                     scales=hl_sc[:, 512 * g : 512 * g + 512],
                     in_=hlgs[g][:],
                 )
+
+        hl_t = keep.tile([P, NJ, NODES], BF16, name="hl_t")
+
+        def turned_mm(g, j):
+            yb = ypool.tile([P, 512], F32, name="yb", tag="y")
+            s1b[(g, j)] = yb
+            nc.tensor.matmul_mx(
+                out=yb[:],
+                lhsT=w_codes[:, 128 * j : 128 * j + 128].bitcast(FP8X4),
+                lhsT_scale=w_sc[:, 128 * j : 128 * j + 128],
+                rhs=h_codes[:, 512 * g : 512 * g + 512].bitcast(FP8X4),
+                rhs_scale=h_sc[:, 512 * g : 512 * g + 512],
+                start=True,
+                stop=True,
+            )
+
+        def turned_bias(g, j):
+            nc.scalar.activation(
+                out=hl_t[:, j, 512 * g : 512 * g + 512], in_=s1b[(g, j)][:], func=ACT.Identity,
+                bias=gb[:, 8 + j : 9 + j],
+            )
+
+        def turned_transposes(g, half):
+            tu = ring.tile([P, 512], F32, name="tu", tag="ring")
+            s1b[(g, half, "t")] = tu
+            for u in range(2):
+                for j2 in range(2):
+                    lo = 256 * g + 128 * u
+                    nc.tensor.transpose(
+                        tu[:, 256 * u + 128 * j2 : 256 * u + 128 * j2 + 128],
+                        hl_t[:, 2 * half + j2, :].bitcast(F32)[:, lo : lo + 128],
+                        ident_f[:],
+                    )
+
+        def turned_words(g, half):
+            if half == 0:
+                hlgs[g] = hlgp.tile([P, 4 * FEAT], BF16, name="hlg", tag="hlg", align_bytes=64)
+            nc.scalar.copy(
+                out=hlgs[g][:].bitcast(F32)[:, 512 * half : 512 * half + 512].rearrange("p (f u) -> p f u", u=2),
+                in_=s1b[(g, half, "t")][:].rearrange("p (u f) -> p f u", u=2),
+            )
 
         zs = keep.tile([P, NJ, NODES], F32, name="zs")
         junk_s = zs[:, 0, 0 : NODES // 2].bitcast(BF16)
@@ -227,11 +252,17 @@ def tile_gcnlayer_kernel(tc, h, adj, W, b, bn_weight, bn_bias, res_weight, out):
         def spread_copy(c):
             nc.scalar.copy(out=d_sb[:, 512 * c : 512 * c + 512], in_=dps[c][:])
 
-        ah = keep.tile([P, NT * NODES], BF16, name="ah")
+        ah = a_sb
         ah32 = ah[:].bitcast(F32)
         a_codes = keep.tile([P, NG, NODES], U32, name="a_codes", align_bytes=64)
         a_sc = keep.tile([P, NG, NODES], U8, name="a_sc", align_bytes=64)
-        st = const.tile([P, NJ, NG, 6], F32, name="st")
+        first_tuple = [sum(1 if k in SCALAR_STATS else 2 for k in range(c)) for c in range(NG + 1)]
+        st = const.tile([P, NJ, first_tuple[NG], 3], F32, name="st")
+        for c in SCALAR_STATS:
+            nc.vector.memset(st[:, :, first_tuple[c], 0], 512.0)
+        sums = const.tile([P, 2, NJ], F32, name="sums")
+        negm = const.tile([P, 2, NJ], F32, name="negm")
+        sq = keep.tile([P, 512], F32, name="sq")
         tus, grps, ybs = {}, {}, {}
 
         def scale_on_vector(i, g):
@@ -293,7 +324,8 @@ def tile_gcnlayer_kernel(tc, h, adj, W, b, bn_weight, bn_bias, res_weight, out):
         def unit_words(c, g, half):
             if half == 0:
                 grps[(c, g)] = gpool.tile([P, 2048], BF16, name="grp", tag="grp", align_bytes=64)
-            nc.scalar.copy(
+            copy = nc.vector.tensor_copy if (half == 1 and (3 * c + g) in VECTOR_WORDS) else nc.scalar.copy
+            copy(
                 out=grps[(c, g)][:].bitcast(F32)[:, 512 * half : 512 * half + 512].rearrange(
                     "p (m u) -> p m u", u=2
                 ),
@@ -319,18 +351,38 @@ def tile_gcnlayer_kernel(tc, h, adj, W, b, bn_weight, bn_bias, res_weight, out):
                 stop=(g == NG - 1),
             )
 
-        def chunk_matmuls(c):
+        cmb = {}
+
+        def chunk_mm(c, j):
+            yb = ypool.tile([P, 512], F32, name="yb", tag="y")
+            cmb[(c, j)] = yb
+            for g in range(NG):
+                one_pass(yb, c, g, j)
+
+        def chunk_cp(c, j):
             cs = slice(512 * c, 512 * c + 512)
-            for j in range(NJ):
-                yb = ypool.tile([P, 512], F32, name="yb", tag="y")
-                for g in range(NG):
-                    one_pass(yb, c, g, j)
-                nc.scalar.copy(out=zs[:, j, cs], in_=yb[:])
+            nc.scalar.activation(
+                out=zs[:, j, cs], in_=cmb[(c, j)][:], func=ACT.Copy, accum_out=sums[:, c, j : j + 1]
+            )
 
         def chunk_stats(c):
             cs = slice(512 * c, 512 * c + 512)
+            k = first_tuple[c]
+            if c == NG - 1:
+                for j in range(NJ):
+                    nc.vector.bn_stats(out=st[:, j, k : k + 2, :].rearrange("p a b -> p (a b)"), in_=ybs[j][:])
+                return
+            if c not in SCALAR_STATS:
+                for j in range(NJ):
+                    nc.vector.bn_stats(out=st[:, j, k : k + 2, :].rearrange("p a b -> p (a b)"), in_=zs[:, j, cs])
+                return
+            nc.scalar.mul(out=negm[:, c, :], in_=sums[:, c, :], mul=-1.0 / 512.0)
+            nc.scalar.mul(out=st[:, :, k, 1], in_=sums[:, c, :], mul=1.0 / 512.0)
             for j in range(NJ):
-                nc.vector.bn_stats(out=st[:, j, c, :], in_=(zs[:, j, cs] if c < NG - 1 else ybs[j][:]))
+                nc.scalar.activation(
+                    out=sq[:], in_=zs[:, j, cs], func=ACT.Square, bias=negm[:, c, j : j + 1],
+                    accum_out=st[:, j, k, 2:3],
+                )
 
         def last_chunk_banks():
             ybs[0] = ypool.tile([P, 512], F32, name="yb", tag="y")
@@ -342,64 +394,189 @@ def tile_gcnlayer_kernel(tc, h, adj, W, b, bn_weight, bn_bias, res_weight, out):
             for j in range(NJ):
                 one_pass(ybs[j], NG - 1, g, j)
 
-        def front(c, g):
-            for half in range(2):
-                unit_scale(c, g, half)
-                unit_transposes(c, g, half)
-                unit_words(c, g, half)
+        def scale_tile(c, g, t):
+            if t in POOL_TILES:
+                scale_on_pool(4 * c + t, g)
+            else:
+                scale_on_vector(4 * c + t, g)
 
         stage0_w()
         stage0_h(0)
+        stage0_hq(0)
         small_vectors()
         stage0_h(1)
-        for k in range(4):
-            stage1_piece(k)
+        stage0_hq(1)
         stage0_h(2)
-        for i in range(4):
-            row_sum(i)
-            diag_block(i)
-            stage1_piece(4 + i)
+        stage0_hq(2)
+        row_sum(0)
+        diag_block(0)
+        row_sum(1)
+        diag_block(1)
+        turned_mm(0, 0)
+        turned_mm(0, 1)
+        turned_bias(0, 0)
+        turned_bias(0, 1)
+        turned_mm(0, 2)
+        turned_mm(0, 3)
+        turned_bias(0, 2)
+        turned_bias(0, 3)
+        turned_transposes(0, 0)
+        turned_words(0, 0)
+        turned_transposes(0, 1)
+        turned_words(0, 1)
+        row_sum(2)
+        diag_block(2)
+        row_sum(3)
+        diag_block(3)
         dis_group(0)
         spread_matmuls(0)
+        row_sum(4)
+        diag_block(4)
+        row_sum(5)
+        diag_block(5)
+        row_sum(6)
+        diag_block(6)
         spread_copy(0)
-        for i in range(4, 8):
-            row_sum(i)
-            diag_block(i)
-            stage1_piece(4 + i)
+        row_sum(7)
+        diag_block(7)
         dis_group(1)
         spread_matmuls(1)
-        spread_copy(1)
-        front(0, 0)
         row_sum(8)
         diag_block(8)
         row_sum(9)
         diag_block(9)
-        front(0, 1)
-        unit_quant(0, 0)
         row_sum(10)
         diag_block(10)
+        spread_copy(1)
         row_sum(11)
         diag_block(11)
         dis_group(2)
         spread_matmuls(2)
+        stage1_quant(0)
+        scale_tile(0, 0, 3)
+        scale_tile(0, 0, 0)
+        scale_tile(0, 0, 1)
+        unit_transposes(0, 0, 0)
+        unit_words(0, 0, 0)
+        scale_tile(0, 0, 2)
+        unit_transposes(0, 0, 1)
+        unit_words(0, 0, 1)
         spread_copy(2)
-        front(1, 0)
+        turned_mm(1, 0)
+        turned_mm(1, 1)
+        turned_bias(1, 0)
+        turned_bias(1, 1)
+        turned_mm(1, 2)
+        turned_mm(1, 3)
+        turned_bias(1, 2)
+        turned_bias(1, 3)
+        turned_transposes(1, 0)
+        turned_words(1, 0)
+        turned_transposes(1, 1)
+        turned_words(1, 1)
+        scale_tile(0, 1, 3)
+        scale_tile(0, 1, 0)
+        scale_tile(0, 1, 1)
+        unit_transposes(0, 1, 0)
+        unit_words(0, 1, 0)
+        scale_tile(0, 1, 2)
+        unit_transposes(0, 1, 1)
+        unit_words(0, 1, 1)
+        unit_quant(0, 0)
+        stage1_quant(1)
+        turned_mm(2, 0)
+        turned_mm(2, 1)
+        turned_bias(2, 0)
+        turned_bias(2, 1)
+        turned_mm(2, 2)
+        turned_mm(2, 3)
+        turned_bias(2, 2)
+        turned_bias(2, 3)
+        turned_transposes(2, 0)
+        turned_words(2, 0)
+        turned_transposes(2, 1)
+        turned_words(2, 1)
+        scale_tile(0, 2, 3)
+        scale_tile(0, 2, 0)
+        scale_tile(0, 2, 1)
+        unit_transposes(0, 2, 0)
+        unit_words(0, 2, 0)
+        scale_tile(0, 2, 2)
+        unit_transposes(0, 2, 1)
+        unit_words(0, 2, 1)
         unit_quant(0, 1)
-        front(1, 1)
-        unit_quant(1, 0)
-        front(0, 2)
-        unit_quant(1, 1)
-        front(1, 2)
+        stage1_quant(2)
+        scale_tile(1, 0, 3)
+        scale_tile(1, 0, 0)
+        scale_tile(1, 0, 1)
+        unit_transposes(1, 0, 0)
+        unit_words(1, 0, 0)
+        scale_tile(1, 0, 2)
+        unit_transposes(1, 0, 1)
+        unit_words(1, 0, 1)
         unit_quant(0, 2)
-        chunk_matmuls(0)
-        front(2, 0)
-        unit_quant(1, 2)
-        chunk_matmuls(1)
+        chunk_mm(0, 0)
+        chunk_cp(0, 0)
+        chunk_mm(0, 1)
+        chunk_cp(0, 1)
+        chunk_mm(0, 2)
+        chunk_cp(0, 2)
+        chunk_mm(0, 3)
+        chunk_cp(0, 3)
+        scale_tile(1, 1, 3)
+        scale_tile(1, 1, 0)
+        scale_tile(1, 1, 1)
+        unit_transposes(1, 1, 0)
+        unit_words(1, 1, 0)
+        scale_tile(1, 1, 2)
+        unit_transposes(1, 1, 1)
+        unit_words(1, 1, 1)
+        unit_quant(1, 0)
         chunk_stats(0)
-        front(2, 1)
+        scale_tile(1, 2, 3)
+        scale_tile(1, 2, 0)
+        scale_tile(1, 2, 1)
+        unit_transposes(1, 2, 0)
+        unit_words(1, 2, 0)
+        scale_tile(1, 2, 2)
+        unit_transposes(1, 2, 1)
+        unit_words(1, 2, 1)
+        unit_quant(1, 1)
+        scale_tile(2, 0, 3)
+        scale_tile(2, 0, 0)
+        scale_tile(2, 0, 1)
+        unit_transposes(2, 0, 0)
+        unit_words(2, 0, 0)
+        scale_tile(2, 0, 2)
+        unit_transposes(2, 0, 1)
+        unit_words(2, 0, 1)
+        unit_quant(1, 2)
+        chunk_mm(1, 0)
+        chunk_cp(1, 0)
+        chunk_mm(1, 1)
+        chunk_cp(1, 1)
+        chunk_mm(1, 2)
+        chunk_cp(1, 2)
+        chunk_mm(1, 3)
+        chunk_cp(1, 3)
+        scale_tile(2, 1, 3)
+        scale_tile(2, 1, 0)
+        scale_tile(2, 1, 1)
+        unit_transposes(2, 1, 0)
+        unit_words(2, 1, 0)
+        scale_tile(2, 1, 2)
+        unit_transposes(2, 1, 1)
+        unit_words(2, 1, 1)
         unit_quant(2, 0)
-        front(2, 2)
         chunk_stats(1)
+        scale_tile(2, 2, 3)
+        scale_tile(2, 2, 0)
+        scale_tile(2, 2, 1)
+        unit_transposes(2, 2, 0)
+        unit_words(2, 2, 0)
+        scale_tile(2, 2, 2)
+        unit_transposes(2, 2, 1)
+        unit_words(2, 2, 1)
         last_chunk_banks()
         last_chunk_matmuls(0)
         unit_quant(2, 1)
@@ -420,36 +597,15 @@ def tile_gcnlayer_kernel(tc, h, adj, W, b, bn_weight, bn_bias, res_weight, out):
         sh = const.tile([P, NJ], F32, name="sh")
         nc.vector.tensor_tensor(out=sh[:], in0=gb[:, 4:8], in1=ms[:], op=ALU.subtract)
 
-        def normalise(c, j, eng):
-            cs = slice(512 * c, 512 * c + 512)
-            if eng == "S":
-                nc.scalar.activation(
-                    out=zs[:, j, cs],
-                    in_=(zs[:, j, cs] if c < NG - 1 else ybs[j][:]),
-                    func=ACT.Relu,
-                    scale=sc[:, j : j + 1],
-                    bias=sh[:, j : j + 1],
-                )
-            else:
-                nc.vector.tensor_scalar(
-                    out=zs[:, j, cs],
-                    in0=zs[:, j, cs],
-                    scalar1=sc[:, j : j + 1],
-                    scalar2=sh[:, j : j + 1],
-                    op0=ALU.mult,
-                    op1=ALU.add,
-                )
-                nc.vector.tensor_scalar(
-                    out=zs[:, j, cs], in0=zs[:, j, cs], scalar1=0.0, scalar2=None, op0=ALU.max
-                )
+        def normalise(j, lo, hi):
+            src = zs[:, j, lo:hi] if lo < 1024 else ybs[j][:, lo - 1024 : hi - 1024]
+            nc.scalar.activation(
+                out=zs[:, j, lo:hi], in_=src, func=ACT.Relu, scale=sc[:, j : j + 1], bias=sh[:, j : j + 1]
+            )
 
-        normalise(0, 0, "S")
-        normalise(0, 1, "S")
-        normalise(0, 2, "V")
-        normalise(0, 3, "V")
-        for c in (1, 2):
+        for lo, hi in NORMALISE_PIECES:
             for j in range(NJ):
-                normalise(c, j, "S")
+                normalise(j, lo, hi)
 
         for i in range(NT):
             ob = ring.tile([P, FEAT], F32, name="ob", tag="ring")

@@ -18,11 +18,12 @@ NT = NODES // P
 NG = NODES // 512
 NJ = FEAT // P
 BN_EPS = 1e-5
-VECTOR_ROW_SUMS = (0, 1, 3, 4, 5, 7, 8, 9, 11)
-POOL_TILES = (3,)
+CHUNKS = ((0, 4), (4, 4), (8, 2), (10, 2))
+LAST = len(CHUNKS) - 1
+SCALAR_ROW_SUMS = (2, 6, 10)
+POOL_ROW_TILES = (3, 7)
 SCALAR_STATS = (0,)
-NORMALISE_PIECES = ((0, 128), (128, 512), (512, 1024), (1024, 1536))
-VECTOR_WORDS = ()
+NORMALISE_PIECES = ((0, 512), (512, 1024), (1024, 1280), (1280, 1536))
 
 FLOPS = 2 * NODES * FEAT * FEAT + 2 * NODES * NODES * FEAT
 
@@ -62,6 +63,7 @@ def tile_gcnlayer_kernel(tc, h, adj, W, b, bn_weight, bn_bias, res_weight, out):
                 out=a_sb[:, 2 * NODES * w : 2 * NODES * (w + 1)].rearrange("q (t n) -> q t n", t=2),
                 in_=adj_v[:, 2 * w : 2 * w + 2, :],
             )
+        a32 = a_sb[:].bitcast(F32)
 
         ident_f = const.tile([P, P], F32, name="ident_f")
         make_identity(nc, ident_f[:])
@@ -93,28 +95,17 @@ def tile_gcnlayer_kernel(tc, h, adj, W, b, bn_weight, bn_bias, res_weight, out):
             nc.tensor.matmul(out=rp[:], lhsT=ones[:], rhs=zr[:], start=True, stop=True)
             nc.vector.tensor_copy(out=res_f[:], in_=rp[:, 0:1])
 
-        def words_to_k(src32, pair, grouped32, eng, split_rows):
-            xt = ring.tile([P, 512], F32, name="xt", tag="ring")
-            for r2 in range(2):
-                for u in range(2):
-                    lo = 256 * (2 * pair + r2) + 128 * u
+        def turn_words(src32, columns, dst32, copy):
+            tu = ring.tile([P, 512], F32, name="tu", tag="ring")
+            for u in range(2):
+                for r2 in range(2):
                     nc.tensor.transpose(
-                        xt[:, 256 * u + 128 * r2 : 256 * u + 128 * r2 + 128],
-                        src32[:, lo : lo + 128],
-                        ident_f[:],
+                        tu[:, 256 * u + 128 * r2 : 256 * u + 128 * r2 + 128], src32(r2)[:, columns(u)], ident_f[:]
                     )
-            copy = nc.scalar.copy if eng == "S" else nc.vector.tensor_copy
-            dst = grouped32[:, 512 * pair : 512 * pair + 512]
-            if split_rows:
-                copy(
-                    out=dst.rearrange("p (e q u) -> p e q u", e=2, u=2),
-                    in_=xt[:].rearrange("p (u q e) -> p e q u", u=2, e=2),
-                )
-            else:
-                copy(
-                    out=dst.rearrange("p (r u) -> p r u", u=2),
-                    in_=xt[:].rearrange("p (u r) -> p r u", u=2),
-                )
+            copy(
+                out=dst32.rearrange("p (r u) -> p r u", u=2),
+                in_=tu[:].rearrange("p (u r) -> p r u", u=2),
+            )
 
         wg = keep.tile([P, 4 * FEAT], BF16, name="wg", align_bytes=64)
         w_codes = keep.tile([P, FEAT], U32, name="w_codes", align_bytes=64)
@@ -123,75 +114,60 @@ def tile_gcnlayer_kernel(tc, h, adj, W, b, bn_weight, bn_bias, res_weight, out):
         h_codes = keep.tile([P, NODES], U32, name="h_codes", align_bytes=64)
         h_sc = keep.tile([P, NODES], U8, name="h_sc", align_bytes=64)
 
+        def rows_to_k(src, pair, grouped, copy):
+            s32 = src[:].bitcast(F32)
+            turn_words(
+                lambda r2: s32[:, 256 * (2 * pair + r2) : 256 * (2 * pair + r2) + 256],
+                lambda u: slice(128 * u, 128 * u + 128),
+                grouped[:].bitcast(F32)[:, 512 * pair : 512 * pair + 512],
+                copy,
+            )
+
         def stage0_w():
-            for pair in range(2):
-                words_to_k(w_sb[:].bitcast(F32), pair, wg[:].bitcast(F32), "SV"[pair], False)
+            rows_to_k(w_sb, 0, wg, nc.scalar.copy)
+            rows_to_k(w_sb, 1, wg, nc.vector.tensor_copy)
             nc.vector.quantize_mx(out=w_codes[:].bitcast(FP8X4), scales=w_sc[:], in_=wg[:])
 
         def stage0_h(g):
             for pair in (2 * g, 2 * g + 1):
-                words_to_k(h_sb[:].bitcast(F32), pair, hg[:].bitcast(F32), "S", False)
-
-        def stage0_hq(g):
+                rows_to_k(h_sb, pair, hg, nc.scalar.copy)
             nc.vector.quantize_mx(
                 out=h_codes[:, 512 * g : 512 * g + 512].bitcast(FP8X4),
                 scales=h_sc[:, 512 * g : 512 * g + 512],
                 in_=hg[:, 2048 * g : 2048 * g + 2048],
             )
 
+        hl_t = keep.tile([P, NJ, NODES], BF16, name="hl_t")
         hl_codes = keep.tile([P, NG * FEAT], U32, name="hl_codes", align_bytes=64)
         hl_sc = keep.tile([P, NG * FEAT], U8, name="hl_sc", align_bytes=64)
-        hlgs = {}
 
-        s1b = {}
-
-        def stage1_quant(g):
-            if True:
-                nc.vector.quantize_mx(
-                    out=hl_codes[:, 512 * g : 512 * g + 512].bitcast(FP8X4),
-                    scales=hl_sc[:, 512 * g : 512 * g + 512],
-                    in_=hlgs[g][:],
+        def stage1(g):
+            for j in range(NJ):
+                yb = ypool.tile([P, 512], F32, name="yb", tag="y")
+                nc.tensor.matmul_mx(
+                    out=yb[:],
+                    lhsT=w_codes[:, 128 * j : 128 * j + 128].bitcast(FP8X4),
+                    lhsT_scale=w_sc[:, 128 * j : 128 * j + 128],
+                    rhs=h_codes[:, 512 * g : 512 * g + 512].bitcast(FP8X4),
+                    rhs_scale=h_sc[:, 512 * g : 512 * g + 512],
+                    start=True,
+                    stop=True,
                 )
-
-        hl_t = keep.tile([P, NJ, NODES], BF16, name="hl_t")
-
-        def turned_mm(g, j):
-            yb = ypool.tile([P, 512], F32, name="yb", tag="y")
-            s1b[(g, j)] = yb
-            nc.tensor.matmul_mx(
-                out=yb[:],
-                lhsT=w_codes[:, 128 * j : 128 * j + 128].bitcast(FP8X4),
-                lhsT_scale=w_sc[:, 128 * j : 128 * j + 128],
-                rhs=h_codes[:, 512 * g : 512 * g + 512].bitcast(FP8X4),
-                rhs_scale=h_sc[:, 512 * g : 512 * g + 512],
-                start=True,
-                stop=True,
-            )
-
-        def turned_bias(g, j):
-            nc.scalar.activation(
-                out=hl_t[:, j, 512 * g : 512 * g + 512], in_=s1b[(g, j)][:], func=ACT.Identity,
-                bias=gb[:, 8 + j : 9 + j],
-            )
-
-        def turned_transposes(g, half):
-            tu = ring.tile([P, 512], F32, name="tu", tag="ring")
-            s1b[(g, half, "t")] = tu
-            for u in range(2):
-                for j2 in range(2):
-                    lo = 256 * g + 128 * u
-                    nc.tensor.transpose(
-                        tu[:, 256 * u + 128 * j2 : 256 * u + 128 * j2 + 128],
-                        hl_t[:, 2 * half + j2, :].bitcast(F32)[:, lo : lo + 128],
-                        ident_f[:],
-                    )
-
-        def turned_words(g, half):
-            if half == 0:
-                hlgs[g] = hlgp.tile([P, 4 * FEAT], BF16, name="hlg", tag="hlg", align_bytes=64)
-            nc.scalar.copy(
-                out=hlgs[g][:].bitcast(F32)[:, 512 * half : 512 * half + 512].rearrange("p (f u) -> p f u", u=2),
-                in_=s1b[(g, half, "t")][:].rearrange("p (u f) -> p f u", u=2),
+                nc.scalar.activation(
+                    out=hl_t[:, j, 512 * g : 512 * g + 512], in_=yb[:], func=ACT.Identity, bias=gb[:, 8 + j : 9 + j]
+                )
+            hlg = hlgp.tile([P, 4 * FEAT], BF16, name="hlg", tag="hlg", align_bytes=64)
+            for half in range(2):
+                turn_words(
+                    lambda j2: hl_t[:, 2 * half + j2, :].bitcast(F32),
+                    lambda u: slice(256 * g + 128 * u, 256 * g + 128 * u + 128),
+                    hlg[:].bitcast(F32)[:, 512 * half : 512 * half + 512],
+                    nc.scalar.copy,
+                )
+            nc.vector.quantize_mx(
+                out=hl_codes[:, 512 * g : 512 * g + 512].bitcast(FP8X4),
+                scales=hl_sc[:, 512 * g : 512 * g + 512],
+                in_=hlg[:],
             )
 
         zs = keep.tile([P, NJ, NODES], F32, name="zs")
@@ -201,9 +177,14 @@ def tile_gcnlayer_kernel(tc, h, adj, W, b, bn_weight, bn_bias, res_weight, out):
         dis = const.tile([P, NT], F32, name="dis")
         d_sb = keep.tile([P, NODES], F32, name="d_sb")
         adj_i = keep.tile([P, NT, P], F32, name="adj_i")
+        dps = {}
 
         def row_sum(i):
-            if i in VECTOR_ROW_SUMS:
+            if i in SCALAR_ROW_SUMS:
+                nc.scalar.activation(
+                    out=junk_s, in_=a_sb[:, NODES * i : NODES * (i + 1)], func=ACT.Copy, accum_out=deg[:, i : i + 1]
+                )
+            else:
                 nc.vector.tensor_scalar(
                     out=junk_v,
                     in0=a_sb[:, NODES * i : NODES * (i + 1)],
@@ -213,62 +194,56 @@ def tile_gcnlayer_kernel(tc, h, adj, W, b, bn_weight, bn_bias, res_weight, out):
                     op1=ALU.add,
                     accum_out=deg[:, i : i + 1],
                 )
-            else:
-                nc.scalar.activation(
-                    out=junk_s,
-                    in_=a_sb[:, NODES * i : NODES * (i + 1)],
-                    func=ACT.Copy,
-                    accum_out=deg[:, i : i + 1],
-                )
-
-        def diag_block(i):
             lo = NODES * i + P * i
-            nc.gpsimd.tensor_tensor(
-                out=adj_i[:, i, :], in0=a_sb[:, lo : lo + P], in1=ident_f[:], op=ALU.add
-            )
+            nc.gpsimd.tensor_tensor(out=adj_i[:, i, :], in0=a_sb[:, lo : lo + P], in1=ident_f[:], op=ALU.add)
 
-        def dis_group(c):
+        def spread(g):
             nc.scalar.activation(
-                out=dis[:, 4 * c : 4 * c + 4],
-                in_=deg[:, 4 * c : 4 * c + 4],
-                func=ACT.Abs_reciprocal_sqrt,
-                bias=one1[:, 0:1],
+                out=dis[:, 4 * g : 4 * g + 4], in_=deg[:, 4 * g : 4 * g + 4], func=ACT.Abs_reciprocal_sqrt, bias=one1[:, 0:1]
             )
-
-        dps = {}
-
-        def spread_matmuls(c):
-            dp = dpool.tile([P, 512], F32, name="dp%d" % c, tag="d%d" % c)
-            dps[c] = dp
+            dp = dpool.tile([P, 512], F32, name="dp%d" % g, tag="d%d" % g)
+            dps[g] = dp
             for t in range(4):
                 nc.tensor.matmul(
                     out=dp[:, 128 * t : 128 * t + 128],
-                    lhsT=dis[:, 4 * c + t : 4 * c + t + 1].to_broadcast([P, P]),
+                    lhsT=dis[:, 4 * g + t : 4 * g + t + 1].to_broadcast([P, P]),
                     rhs=ident_f[:],
                     start=True,
                     stop=True,
                 )
+            nc.scalar.copy(out=d_sb[:, 512 * g : 512 * g + 512], in_=dp[:])
 
-        def spread_copy(c):
-            nc.scalar.copy(out=d_sb[:, 512 * c : 512 * c + 512], in_=dps[c][:])
-
-        ah = a_sb
-        ah32 = ah[:].bitcast(F32)
         a_codes = keep.tile([P, NG, NODES], U32, name="a_codes", align_bytes=64)
         a_sc = keep.tile([P, NG, NODES], U8, name="a_sc", align_bytes=64)
-        first_tuple = [sum(1 if k in SCALAR_STATS else 2 for k in range(c)) for c in range(NG + 1)]
-        st = const.tile([P, NJ, first_tuple[NG], 3], F32, name="st")
+        first_tuple = [sum(1 if k in SCALAR_STATS else 2 for k in range(c)) for c in range(LAST + 2)]
+        st = const.tile([P, NJ, first_tuple[LAST + 1], 3], F32, name="st")
         for c in SCALAR_STATS:
-            nc.vector.memset(st[:, :, first_tuple[c], 0], 512.0)
-        sums = const.tile([P, 2, NJ], F32, name="sums")
-        negm = const.tile([P, 2, NJ], F32, name="negm")
+            nc.vector.memset(st[:, :, first_tuple[c], 0], float(P * CHUNKS[c][1]))
+        sums = const.tile([P, LAST, NJ], F32, name="sums")
+        negm = const.tile([P, LAST, NJ], F32, name="negm")
         sq = keep.tile([P, 512], F32, name="sq")
-        tus, grps, ybs = {}, {}, {}
+        grps, ybs = {}, {}
 
-        def scale_on_vector(i, g):
+        def scale_tile(i, g):
             lo = NODES * i + 512 * g
+            own = P * (i % 4)
+            if i in POOL_ROW_TILES:
+                xs = xpool.tile([P, 512], F32, name="xs", tag="xs")
+                nc.gpsimd.tensor_scalar(
+                    out=xs[:], in0=a_sb[:, lo : lo + 512], scalar1=dis[:, i : i + 1], scalar2=1.0,
+                    op0=ALU.mult, op1=ALU.mult,
+                )
+                if i // 4 == g:
+                    nc.gpsimd.tensor_scalar(
+                        out=xs[:, own : own + P], in0=adj_i[:, i, :], scalar1=dis[:, i : i + 1], scalar2=1.0,
+                        op0=ALU.mult, op1=ALU.mult,
+                    )
+                nc.gpsimd.tensor_tensor(
+                    out=a_sb[:, lo : lo + 512], in0=xs[:], in1=d_sb[:, 512 * g : 512 * g + 512], op=ALU.mult
+                )
+                return
             nc.vector.scalar_tensor_tensor(
-                out=ah[:, lo : lo + 512],
+                out=a_sb[:, lo : lo + 512],
                 in0=a_sb[:, lo : lo + 512],
                 scalar=dis[:, i : i + 1],
                 in1=dps[g][:],
@@ -276,314 +251,126 @@ def tile_gcnlayer_kernel(tc, h, adj, W, b, bn_weight, bn_bias, res_weight, out):
                 op1=ALU.mult,
             )
             if i // 4 == g:
-                lo = NODES * i + P * i
                 nc.vector.scalar_tensor_tensor(
-                    out=ah[:, lo : lo + P],
+                    out=a_sb[:, lo + own : lo + own + P],
                     in0=adj_i[:, i, :],
                     scalar=dis[:, i : i + 1],
-                    in1=dps[g][:, P * (i % 4) : P * (i % 4) + P],
+                    in1=dps[g][:, own : own + P],
                     op0=ALU.mult,
                     op1=ALU.mult,
                 )
 
-        def scale_on_pool(i, g):
-            lo = NODES * i + 512 * g
-            xs = xpool.tile([P, 512], F32, name="xs", tag="xs")
-            nc.gpsimd.tensor_scalar(
-                out=xs[:], in0=a_sb[:, lo : lo + 512], scalar1=dis[:, i : i + 1], scalar2=1.0,
-                op0=ALU.mult, op1=ALU.mult,
-            )
-            if i // 4 == g:
-                nc.gpsimd.tensor_scalar(
-                    out=xs[:, P * (i % 4) : P * (i % 4) + P], in0=adj_i[:, i, :], scalar1=dis[:, i : i + 1],
-                    scalar2=1.0, op0=ALU.mult, op1=ALU.mult,
+        def unit_front(c, g):
+            t0, nt = CHUNKS[c]
+            grp = gpool.tile([P, 512 * nt], BF16, name="grp", tag="grp", align_bytes=64)
+            grps[(c, g)] = grp
+            for i in range(t0, t0 + nt):
+                if i in POOL_ROW_TILES:
+                    scale_tile(i, g)
+            for half in range(nt // 2):
+                for i in (t0 + 2 * half, t0 + 2 * half + 1):
+                    if i not in POOL_ROW_TILES:
+                        scale_tile(i, g)
+                turn_words(
+                    lambda r2: a32[:, 768 * (t0 + 2 * half + r2) : 768 * (t0 + 2 * half + r2) + 768],
+                    lambda u: slice(256 * g + 128 * u, 256 * g + 128 * u + 128),
+                    grp[:].bitcast(F32)[:, 512 * half : 512 * half + 512],
+                    nc.scalar.copy,
                 )
-            nc.gpsimd.tensor_tensor(
-                out=ah[:, lo : lo + 512], in0=xs[:], in1=d_sb[:, 512 * g : 512 * g + 512], op=ALU.mult
-            )
 
-        def unit_scale(c, g, half):
-            for t in (2 * half, 2 * half + 1):
-                if t in POOL_TILES:
-                    scale_on_pool(4 * c + t, g)
-                else:
-                    scale_on_vector(4 * c + t, g)
-
-        def unit_transposes(c, g, half):
-            tu = ring.tile([P, 512], F32, name="tu", tag="ring")
-            tus[(c, g, half)] = tu
-            for u in range(2):
-                for e2 in range(2):
-                    lo = 768 * (4 * c + 2 * half + e2) + 256 * g + 128 * u
-                    nc.tensor.transpose(
-                        tu[:, 256 * u + 128 * e2 : 256 * u + 128 * e2 + 128],
-                        ah32[:, lo : lo + 128],
-                        ident_f[:],
-                    )
-
-        def unit_words(c, g, half):
-            if half == 0:
-                grps[(c, g)] = gpool.tile([P, 2048], BF16, name="grp", tag="grp", align_bytes=64)
-            copy = nc.vector.tensor_copy if (half == 1 and (3 * c + g) in VECTOR_WORDS) else nc.scalar.copy
-            copy(
-                out=grps[(c, g)][:].bitcast(F32)[:, 512 * half : 512 * half + 512].rearrange(
-                    "p (m u) -> p m u", u=2
-                ),
-                in_=tus[(c, g, half)][:].rearrange("p (u m) -> p m u", u=2),
-            )
+        def nodes_of(c):
+            return slice(P * CHUNKS[c][0], P * (CHUNKS[c][0] + CHUNKS[c][1]))
 
         def unit_quant(c, g):
-            cs = slice(512 * c, 512 * c + 512)
             nc.vector.quantize_mx(
-                out=a_codes[:, g, cs].bitcast(FP8X4), scales=a_sc[:, g, cs], in_=grps[(c, g)][:]
+                out=a_codes[:, g, nodes_of(c)].bitcast(FP8X4), scales=a_sc[:, g, nodes_of(c)], in_=grps[(c, g)][:]
             )
 
         def one_pass(yb, c, g, j):
-            cs = slice(512 * c, 512 * c + 512)
             lo = 512 * g + 128 * j
             nc.tensor.matmul_mx(
                 out=yb[:],
                 lhsT=hl_codes[:, lo : lo + 128].bitcast(FP8X4),
                 lhsT_scale=hl_sc[:, lo : lo + 128],
-                rhs=a_codes[:, g, cs].bitcast(FP8X4),
-                rhs_scale=a_sc[:, g, cs],
+                rhs=a_codes[:, g, nodes_of(c)].bitcast(FP8X4),
+                rhs_scale=a_sc[:, g, nodes_of(c)],
                 start=(g == 0),
                 stop=(g == NG - 1),
             )
 
-        cmb = {}
-
-        def chunk_mm(c, j):
-            yb = ypool.tile([P, 512], F32, name="yb", tag="y")
-            cmb[(c, j)] = yb
-            for g in range(NG):
-                one_pass(yb, c, g, j)
-
-        def chunk_cp(c, j):
-            cs = slice(512 * c, 512 * c + 512)
-            nc.scalar.activation(
-                out=zs[:, j, cs], in_=cmb[(c, j)][:], func=ACT.Copy, accum_out=sums[:, c, j : j + 1]
-            )
+        def chunk_matmuls(c):
+            for j in range(NJ):
+                yb = ypool.tile([P, P * CHUNKS[c][1]], F32, name="yb", tag="y")
+                for g in range(NG):
+                    one_pass(yb, c, g, j)
+                nc.scalar.activation(
+                    out=zs[:, j, nodes_of(c)], in_=yb[:], func=ACT.Copy, accum_out=sums[:, c, j : j + 1]
+                )
 
         def chunk_stats(c):
-            cs = slice(512 * c, 512 * c + 512)
             k = first_tuple[c]
-            if c == NG - 1:
-                for j in range(NJ):
-                    nc.vector.bn_stats(out=st[:, j, k : k + 2, :].rearrange("p a b -> p (a b)"), in_=ybs[j][:])
-                return
             if c not in SCALAR_STATS:
                 for j in range(NJ):
-                    nc.vector.bn_stats(out=st[:, j, k : k + 2, :].rearrange("p a b -> p (a b)"), in_=zs[:, j, cs])
+                    nc.vector.bn_stats(
+                        out=st[:, j, k : k + 2, :].rearrange("p a b -> p (a b)"),
+                        in_=(ybs[j][:] if c == LAST else zs[:, j, nodes_of(c)]),
+                    )
                 return
-            nc.scalar.mul(out=negm[:, c, :], in_=sums[:, c, :], mul=-1.0 / 512.0)
-            nc.scalar.mul(out=st[:, :, k, 1], in_=sums[:, c, :], mul=1.0 / 512.0)
+            width = P * CHUNKS[c][1]
+            nc.scalar.mul(out=negm[:, c, :], in_=sums[:, c, :], mul=-1.0 / width)
+            nc.scalar.mul(out=st[:, :, k, 1], in_=sums[:, c, :], mul=1.0 / width)
             for j in range(NJ):
                 nc.scalar.activation(
-                    out=sq[:], in_=zs[:, j, cs], func=ACT.Square, bias=negm[:, c, j : j + 1],
+                    out=sq[:, 0:width], in_=zs[:, j, nodes_of(c)], func=ACT.Square, bias=negm[:, c, j : j + 1],
                     accum_out=st[:, j, k, 2:3],
                 )
 
         def last_chunk_banks():
-            ybs[0] = ypool.tile([P, 512], F32, name="yb", tag="y")
-            ybs[1] = ypool.tile([P, 512], F32, name="yb", tag="y")
-            ybs[2] = dpool.tile([P, 512], F32, name="yd0", tag="d0")
-            ybs[3] = dpool.tile([P, 512], F32, name="yd1", tag="d1")
-
-        def last_chunk_matmuls(g):
-            for j in range(NJ):
-                one_pass(ybs[j], NG - 1, g, j)
-
-        def scale_tile(c, g, t):
-            if t in POOL_TILES:
-                scale_on_pool(4 * c + t, g)
-            else:
-                scale_on_vector(4 * c + t, g)
+            width = P * CHUNKS[LAST][1]
+            ybs[0] = ypool.tile([P, width], F32, name="yb", tag="y")
+            ybs[1] = ypool.tile([P, width], F32, name="yb", tag="y")
+            ybs[2] = dpool.tile([P, width], F32, name="yd0", tag="d0")
+            ybs[3] = dpool.tile([P, width], F32, name="yd1", tag="d1")
 
         stage0_w()
         stage0_h(0)
-        stage0_hq(0)
         small_vectors()
         stage0_h(1)
-        stage0_hq(1)
         stage0_h(2)
-        stage0_hq(2)
         row_sum(0)
-        diag_block(0)
         row_sum(1)
-        diag_block(1)
-        turned_mm(0, 0)
-        turned_mm(0, 1)
-        turned_bias(0, 0)
-        turned_bias(0, 1)
-        turned_mm(0, 2)
-        turned_mm(0, 3)
-        turned_bias(0, 2)
-        turned_bias(0, 3)
-        turned_transposes(0, 0)
-        turned_words(0, 0)
-        turned_transposes(0, 1)
-        turned_words(0, 1)
+        stage1(0)
         row_sum(2)
-        diag_block(2)
         row_sum(3)
-        diag_block(3)
-        dis_group(0)
-        spread_matmuls(0)
-        row_sum(4)
-        diag_block(4)
-        row_sum(5)
-        diag_block(5)
-        row_sum(6)
-        diag_block(6)
-        spread_copy(0)
-        row_sum(7)
-        diag_block(7)
-        dis_group(1)
-        spread_matmuls(1)
-        row_sum(8)
-        diag_block(8)
-        row_sum(9)
-        diag_block(9)
-        row_sum(10)
-        diag_block(10)
-        spread_copy(1)
-        row_sum(11)
-        diag_block(11)
-        dis_group(2)
-        spread_matmuls(2)
-        stage1_quant(0)
-        scale_tile(0, 0, 3)
-        scale_tile(0, 0, 0)
-        scale_tile(0, 0, 1)
-        unit_transposes(0, 0, 0)
-        unit_words(0, 0, 0)
-        scale_tile(0, 0, 2)
-        unit_transposes(0, 0, 1)
-        unit_words(0, 0, 1)
-        spread_copy(2)
-        turned_mm(1, 0)
-        turned_mm(1, 1)
-        turned_bias(1, 0)
-        turned_bias(1, 1)
-        turned_mm(1, 2)
-        turned_mm(1, 3)
-        turned_bias(1, 2)
-        turned_bias(1, 3)
-        turned_transposes(1, 0)
-        turned_words(1, 0)
-        turned_transposes(1, 1)
-        turned_words(1, 1)
-        scale_tile(0, 1, 3)
-        scale_tile(0, 1, 0)
-        scale_tile(0, 1, 1)
-        unit_transposes(0, 1, 0)
-        unit_words(0, 1, 0)
-        scale_tile(0, 1, 2)
-        unit_transposes(0, 1, 1)
-        unit_words(0, 1, 1)
-        unit_quant(0, 0)
-        stage1_quant(1)
-        turned_mm(2, 0)
-        turned_mm(2, 1)
-        turned_bias(2, 0)
-        turned_bias(2, 1)
-        turned_mm(2, 2)
-        turned_mm(2, 3)
-        turned_bias(2, 2)
-        turned_bias(2, 3)
-        turned_transposes(2, 0)
-        turned_words(2, 0)
-        turned_transposes(2, 1)
-        turned_words(2, 1)
-        scale_tile(0, 2, 3)
-        scale_tile(0, 2, 0)
-        scale_tile(0, 2, 1)
-        unit_transposes(0, 2, 0)
-        unit_words(0, 2, 0)
-        scale_tile(0, 2, 2)
-        unit_transposes(0, 2, 1)
-        unit_words(0, 2, 1)
-        unit_quant(0, 1)
-        stage1_quant(2)
-        scale_tile(1, 0, 3)
-        scale_tile(1, 0, 0)
-        scale_tile(1, 0, 1)
-        unit_transposes(1, 0, 0)
-        unit_words(1, 0, 0)
-        scale_tile(1, 0, 2)
-        unit_transposes(1, 0, 1)
-        unit_words(1, 0, 1)
-        unit_quant(0, 2)
-        chunk_mm(0, 0)
-        chunk_cp(0, 0)
-        chunk_mm(0, 1)
-        chunk_cp(0, 1)
-        chunk_mm(0, 2)
-        chunk_cp(0, 2)
-        chunk_mm(0, 3)
-        chunk_cp(0, 3)
-        scale_tile(1, 1, 3)
-        scale_tile(1, 1, 0)
-        scale_tile(1, 1, 1)
-        unit_transposes(1, 1, 0)
-        unit_words(1, 1, 0)
-        scale_tile(1, 1, 2)
-        unit_transposes(1, 1, 1)
-        unit_words(1, 1, 1)
-        unit_quant(1, 0)
-        chunk_stats(0)
-        scale_tile(1, 2, 3)
-        scale_tile(1, 2, 0)
-        scale_tile(1, 2, 1)
-        unit_transposes(1, 2, 0)
-        unit_words(1, 2, 0)
-        scale_tile(1, 2, 2)
-        unit_transposes(1, 2, 1)
-        unit_words(1, 2, 1)
-        unit_quant(1, 1)
-        scale_tile(2, 0, 3)
-        scale_tile(2, 0, 0)
-        scale_tile(2, 0, 1)
-        unit_transposes(2, 0, 0)
-        unit_words(2, 0, 0)
-        scale_tile(2, 0, 2)
-        unit_transposes(2, 0, 1)
-        unit_words(2, 0, 1)
-        unit_quant(1, 2)
-        chunk_mm(1, 0)
-        chunk_cp(1, 0)
-        chunk_mm(1, 1)
-        chunk_cp(1, 1)
-        chunk_mm(1, 2)
-        chunk_cp(1, 2)
-        chunk_mm(1, 3)
-        chunk_cp(1, 3)
-        scale_tile(2, 1, 3)
-        scale_tile(2, 1, 0)
-        scale_tile(2, 1, 1)
-        unit_transposes(2, 1, 0)
-        unit_words(2, 1, 0)
-        scale_tile(2, 1, 2)
-        unit_transposes(2, 1, 1)
-        unit_words(2, 1, 1)
-        unit_quant(2, 0)
-        chunk_stats(1)
-        scale_tile(2, 2, 3)
-        scale_tile(2, 2, 0)
-        scale_tile(2, 2, 1)
-        unit_transposes(2, 2, 0)
-        unit_words(2, 2, 0)
-        scale_tile(2, 2, 2)
-        unit_transposes(2, 2, 1)
-        unit_words(2, 2, 1)
-        last_chunk_banks()
-        last_chunk_matmuls(0)
-        unit_quant(2, 1)
-        last_chunk_matmuls(1)
-        unit_quant(2, 2)
-        last_chunk_matmuls(2)
-        chunk_stats(2)
+        spread(0)
+        for i in range(4, 8):
+            row_sum(i)
+        spread(1)
+        for i in range(8, 12):
+            row_sum(i)
+        spread(2)
+        units = [(c, g) for c in range(LAST + 1) for g in range(NG)]
+        for k, (c, g) in enumerate(units):
+            unit_front(c, g)
+            if k in (0, 1):
+                stage1(k + 1)
+            if k == 0:
+                continue
+            pc, pg = units[k - 1]
+            if (pc, pg) == (LAST, 0):
+                last_chunk_banks()
+            unit_quant(pc, pg)
+            if pc == LAST:
+                for j in range(NJ):
+                    one_pass(ybs[j], pc, pg, j)
+            elif pg == NG - 1:
+                chunk_matmuls(pc)
+            if pg == 0 and pc > 0:
+                chunk_stats(pc - 1)
+        unit_quant(LAST, NG - 1)
+        for j in range(NJ):
+            one_pass(ybs[j], LAST, NG - 1, j)
+        chunk_stats(LAST)
 
         mv = const.tile([P, NJ, 2], F32, name="mv")
         for j in range(NJ):
@@ -597,15 +384,25 @@ def tile_gcnlayer_kernel(tc, h, adj, W, b, bn_weight, bn_bias, res_weight, out):
         sh = const.tile([P, NJ], F32, name="sh")
         nc.vector.tensor_tensor(out=sh[:], in0=gb[:, 4:8], in1=ms[:], op=ALU.subtract)
 
-        def normalise(j, lo, hi):
-            src = zs[:, j, lo:hi] if lo < 1024 else ybs[j][:, lo - 1024 : hi - 1024]
-            nc.scalar.activation(
-                out=zs[:, j, lo:hi], in_=src, func=ACT.Relu, scale=sc[:, j : j + 1], bias=sh[:, j : j + 1]
-            )
-
+        kept = P * CHUNKS[LAST][0]
         for lo, hi in NORMALISE_PIECES:
             for j in range(NJ):
-                normalise(j, lo, hi)
+                if lo == 0 and j >= 2:
+                    nc.vector.tensor_scalar(
+                        out=zs[:, j, lo:hi], in0=zs[:, j, lo:hi], scalar1=sc[:, j : j + 1], scalar2=sh[:, j : j + 1],
+                        op0=ALU.mult, op1=ALU.add,
+                    )
+                    nc.vector.tensor_scalar(
+                        out=zs[:, j, lo:hi], in0=zs[:, j, lo:hi], scalar1=0.0, scalar2=None, op0=ALU.max
+                    )
+                    continue
+                nc.scalar.activation(
+                    out=zs[:, j, lo:hi],
+                    in_=(zs[:, j, lo:hi] if lo < kept else ybs[j][:, lo - kept : hi - kept]),
+                    func=ACT.Relu,
+                    scale=sc[:, j : j + 1],
+                    bias=sh[:, j : j + 1],
+                )
 
         for i in range(NT):
             ob = ring.tile([P, FEAT], F32, name="ob", tag="ring")

@@ -47,22 +47,37 @@ def tile_gcnlayer_kernel(tc, h, adj, W, b, bn_weight, bn_bias, res_weight, out):
         out_v = out.rearrange("o (t q) f -> q (o t) f", q=P)
 
         w_sb = keep.tile([P, NJ * FEAT], BF16, name="w_sb")
-        nc.sync.dma_start(
-            out=w_sb[:].rearrange("q (r k) -> q r k", r=NJ),
-            in_=W.rearrange("(r q) k -> q r k", q=P),
-        )
         h_sb = keep.tile([P, NT * FEAT], BF16, name="h_sb")
-        for g in range(NG):
+        a_sb = keep.tile([P, (NT + 1) * NODES], BF16, name="a_sb")
+
+        def load_w():
+            nc.sync.dma_start(
+                out=w_sb[:].rearrange("q (r k) -> q r k", r=NJ),
+                in_=W.rearrange("(r q) k -> q r k", q=P),
+            )
+
+        def load_h(g):
             nc.sync.dma_start(
                 out=h_sb[:, 2048 * g : 2048 * g + 2048].rearrange("q (t k) -> q t k", t=4),
                 in_=h_v[:, 4 * g : 4 * g + 4, :],
             )
-        a_sb = keep.tile([P, NT * NODES], BF16, name="a_sb")
-        for w in range(NT // 2):
+
+        def load_adj(w):
             nc.sync.dma_start(
                 out=a_sb[:, 2 * NODES * w : 2 * NODES * (w + 1)].rearrange("q (t n) -> q t n", t=2),
                 in_=adj_v[:, 2 * w : 2 * w + 2, :],
             )
+
+        load_adj(0)
+        load_adj(1)
+        load_w()
+        load_h(0)
+        load_adj(2)
+        load_adj(3)
+        load_adj(4)
+        load_adj(5)
+        load_h(1)
+        load_h(2)
         a32 = a_sb[:].bitcast(F32)
 
         ident_f = const.tile([P, P], F32, name="ident_f")
@@ -194,10 +209,15 @@ def tile_gcnlayer_kernel(tc, h, adj, W, b, bn_weight, bn_bias, res_weight, out):
                     op1=ALU.add,
                     accum_out=deg[:, i : i + 1],
                 )
-            lo = NODES * i + P * i
-            nc.gpsimd.tensor_tensor(out=adj_i[:, i, :], in0=a_sb[:, lo : lo + P], in1=ident_f[:], op=ALU.add)
 
         def spread(g):
+            step = NODES + P
+            nc.gpsimd.tensor_tensor(
+                out=adj_i[:, 4 * g : 4 * g + 4, :],
+                in0=a_sb[:, step * 4 * g : step * (4 * g + 4)].rearrange("q (t x) -> q t x", t=4)[:, :, 0:P],
+                in1=ident_f[:].unsqueeze(1).to_broadcast([P, 4, P]),
+                op=ALU.add,
+            )
             nc.scalar.activation(
                 out=dis[:, 4 * g : 4 * g + 4], in_=deg[:, 4 * g : 4 * g + 4], func=ACT.Abs_reciprocal_sqrt, bias=one1[:, 0:1]
             )

@@ -100,12 +100,14 @@ def tile_gcnlayer_kernel(tc, h, adj, W, b, bn_weight, bn_bias, res_weight, out):
         nc.scalar.activation(out=junk[:], in_=one1[:], func=ACT.Abs_reciprocal_sqrt)
 
         gb = const.tile([P, 12], F32, name="gb")
+        gn = const.tile([P, 2, NJ], F32, name="gn")
         res_f = const.tile([P, 1], F32, name="res_f")
 
         def small_vectors():
             vt_ps = ring.tile([P, P], BF16, name="vt_ps", tag="ring")
             nc.tensor.transpose(vt_ps[:], vt[:], ident_b[:])
             nc.vector.tensor_copy(out=gb[:], in_=vt_ps[:, 0:12])
+            nc.vector.tensor_copy(out=gn[:, 0, :], in_=vt_ps[:, 0:4])
             rp = ring.tile([P, 2], F32, name="rp", tag="ring")
             nc.tensor.matmul(out=rp[:], lhsT=ones[:], rhs=zr[:], start=True, stop=True)
             nc.vector.tensor_copy(out=res_f[:], in_=rp[:, 0:1])
@@ -377,19 +379,15 @@ def tile_gcnlayer_kernel(tc, h, adj, W, b, bn_weight, bn_bias, res_weight, out):
             if k == 0:
                 continue
             pc, pg = units[k - 1]
-            if (pc, pg) == (LAST, 0):
-                last_chunk_banks()
             unit_quant(pc, pg)
-            if pc == LAST:
-                for j in range(NJ):
-                    one_pass(ybs[j], pc, pg, j)
-            elif pg == NG - 1:
-                chunk_matmuls(pc)
-            if pg == 0 and pc > 0:
-                chunk_stats(pc - 1)
+            if g == NG - 1 and c > 0:
+                chunk_matmuls(c - 1)
+                chunk_stats(c - 1)
+        last_chunk_banks()
         unit_quant(LAST, NG - 1)
-        for j in range(NJ):
-            one_pass(ybs[j], LAST, NG - 1, j)
+        for g in range(NG):
+            for j in range(NJ):
+                one_pass(ybs[j], LAST, g, j)
         chunk_stats(LAST)
 
         mv = const.tile([P, NJ, 2], F32, name="mv")
@@ -397,12 +395,14 @@ def tile_gcnlayer_kernel(tc, h, adj, W, b, bn_weight, bn_bias, res_weight, out):
             nc.vector.bn_aggr(out=mv[:, j, :], in_=st[:, j, :, :].rearrange("p c s -> p (c s)"))
         rs = const.tile([P, NJ], F32, name="rs")
         nc.scalar.activation(out=rs[:], in_=mv[:, :, 1], func=ACT.Abs_reciprocal_sqrt, bias=BN_EPS)
-        sc = const.tile([P, NJ], F32, name="sc")
-        nc.vector.tensor_tensor(out=sc[:], in0=gb[:, 0:4], in1=rs[:], op=ALU.mult)
-        ms = const.tile([P, NJ], F32, name="ms")
-        nc.vector.tensor_tensor(out=ms[:], in0=mv[:, :, 0], in1=sc[:], op=ALU.mult)
+        nc.vector.scalar_tensor_tensor(
+            out=gn[:, 1, :], in0=mv[:, :, 0], scalar=-1.0, in1=gb[:, 0:4], op0=ALU.mult, op1=ALU.mult
+        )
+        ss = const.tile([P, 2, NJ], F32, name="ss")
+        nc.vector.tensor_tensor(out=ss[:], in0=gn[:], in1=rs[:].unsqueeze(1).to_broadcast([P, 2, NJ]), op=ALU.mult)
+        sc = ss[:, 0, :]
         sh = const.tile([P, NJ], F32, name="sh")
-        nc.vector.tensor_tensor(out=sh[:], in0=gb[:, 4:8], in1=ms[:], op=ALU.subtract)
+        nc.vector.tensor_tensor(out=sh[:], in0=gb[:, 4:8], in1=ss[:, 1, :], op=ALU.add)
 
         kept = P * CHUNKS[LAST][0]
         for lo, hi in NORMALISE_PIECES:

@@ -325,9 +325,12 @@ def tile_gcnlayer_kernel(tc, h, adj, W, b, bn_weight, bn_bias, res_weight, out):
                 yb = ypool.tile([P, P * CHUNKS[c][1]], F32, name="yb", tag="y")
                 for g in range(NG):
                     one_pass(yb, c, g, j)
-                nc.scalar.activation(
-                    out=zs[:, j, nodes_of(c)], in_=yb[:], func=ACT.Copy, accum_out=sums[:, c, j : j + 1]
-                )
+                if c in SCALAR_STATS:
+                    nc.scalar.activation(
+                        out=zs[:, j, nodes_of(c)], in_=yb[:], func=ACT.Copy, accum_out=sums[:, c, j : j + 1]
+                    )
+                else:
+                    nc.scalar.copy(out=zs[:, j, nodes_of(c)], in_=yb[:])
 
         def chunk_stats(c):
             k = first_tuple[c]

from contextlib import ExitStack

import concourse.mybir as mybir
from concourse.masks import make_identity

F32 = mybir.dt.float32
BF16 = mybir.dt.bfloat16
U8 = mybir.dt.uint8
U32 = mybir.dt.uint32
FP8X4 = mybir.dt.float8_e4m3fn_x4
ALU = mybir.AluOpType
ACT = mybir.ActivationFunctionType

P = 128
NODES = 1536
FEAT = 512
NT = NODES // P
NG = NODES // 512
NJ = FEAT // P
BN_EPS = 1e-5
CHUNKS = ((0, 4), (4, 4), (8, 2), (10, 2))
LAST = len(CHUNKS) - 1
SCALAR_ROW_SUMS = (2, 6, 10)
POOL_ROW_TILES = (3, 7)
SCALAR_STATS = (0,)
NORMALISE_PIECES = ((0, 512), (512, 1024), (1024, 1280), (1280, 1536))

FLOPS = 2 * NODES * FEAT * FEAT + 2 * NODES * NODES * FEAT


def tile_gcnlayer_kernel(tc, h, adj, W, b, bn_weight, bn_bias, res_weight, out):
    nc = tc.nc
    with ExitStack() as ctx:
        ctx.enter_context(tc.manual_schedule(engines={mybir.EngineType.Pool}))
        const = ctx.enter_context(tc.tile_pool(name="const", bufs=1))
        keep = ctx.enter_context(tc.tile_pool(name="keep", bufs=1))
        hlgp = ctx.enter_context(tc.tile_pool(name="hlgp", bufs=2))
        gpool = ctx.enter_context(tc.tile_pool(name="gpool", bufs=3))
        xpool = ctx.enter_context(tc.tile_pool(name="xpool", bufs=2))
        opool = ctx.enter_context(tc.tile_pool(name="opool", bufs=12))
        ring = ctx.enter_context(tc.psum_pool(name="ring", bufs=3))
        ypool = ctx.enter_context(tc.psum_pool(name="ypool", bufs=2))
        dpool = ctx.enter_context(tc.psum_pool(name="dpool", bufs=1))

        h_v = h.rearrange("o (t q) k -> q (o t) k", q=P)
        adj_v = adj.rearrange("o (t q) n -> q (o t) n", q=P)
        out_v = out.rearrange("o (t q) f -> q (o t) f", q=P)

        w_sb = keep.tile([P, NJ * FEAT], BF16, name="w_sb")
        h_sb = keep.tile([P, NT * FEAT], BF16, name="h_sb")
        a_sb = keep.tile([P, (NT + 1) * NODES], BF16, name="a_sb")

        def load_w():
            nc.sync.dma_start(
                out=w_sb[:].rearrange("q (r k) -> q r k", r=NJ),
                in_=W.rearrange("(r q) k -> q r k", q=P),
            )

        def load_h(g):
            nc.sync.dma_start(
                out=h_sb[:, 2048 * g : 2048 * g + 2048].rearrange("q (t k) -> q t k", t=4),
                in_=h_v[:, 4 * g : 4 * g + 4, :],
            )

        def load_adj(w):
            nc.sync.dma_start(
                out=a_sb[:, 2 * NODES * w : 2 * NODES * (w + 1)].rearrange("q (t n) -> q t n", t=2),
                in_=adj_v[:, 2 * w : 2 * w + 2, :],
            )

        load_adj(0)
        load_adj(1)
        load_w()
        load_h(0)
        load_adj(2)
        load_adj(3)
        load_adj(4)
        load_adj(5)
        load_h(1)
        load_h(2)
        a32 = a_sb[:].bitcast(F32)

        ident_f = const.tile([P, P], F32, name="ident_f")
        make_identity(nc, ident_f[:])
        ident_b = const.tile([P, P], BF16, name="ident_b")
        make_identity(nc, ident_b[:])
        ones = const.tile([P, P], BF16, name="ones")
        nc.vector.memset(ones[:], 1.0)
        vt = const.tile([P, P], BF16, name="vt")
        nc.vector.memset(vt[:], 0.0)
        nc.scalar.dma_start(out=vt[0:4, :], in_=bn_weight.rearrange("(j p) -> j p", p=P))
        nc.scalar.dma_start(out=vt[4:8, :], in_=bn_bias.rearrange("(j p) -> j p", p=P))
        nc.scalar.dma_start(out=vt[8:12, :], in_=b.rearrange("(j p) -> j p", p=P))
        zr = const.tile([P, 2], BF16, name="zr")
        nc.vector.memset(zr[:], 0.0)
        nc.scalar.dma_start(out=zr[0:1, 0:1], in_=res_weight.rearrange("(o f) -> o f", o=1))
        one1 = const.tile([P, 1], F32, name="one1")
        nc.vector.memset(one1[:], 1.0)
        junk = const.tile([P, 1], F32, name="junk")
        nc.scalar.activation(out=junk[:], in_=one1[:], func=ACT.Abs_reciprocal_sqrt)

        gb = const.tile([P, 12], F32, name="gb")
        gn = const.tile([P, 2, NJ], F32, name="gn")
        res_f = const.tile([P, 1], F32, name="res_f")

        def small_vectors():
            vt_ps = ring.tile([P, P], BF16, name="vt_ps", tag="ring")
            nc.tensor.transpose(vt_ps[:], vt[:], ident_b[:])
            nc.vector.tensor_copy(out=gb[:], in_=vt_ps[:, 0:12])
            nc.vector.tensor_copy(out=gn[:, 0, :], in_=vt_ps[:, 0:4])
            rp = ring.tile([P, 2], F32, name="rp", tag="ring")
            nc.tensor.matmul(out=rp[:], lhsT=ones[:], rhs=zr[:], start=True, stop=True)
            nc.vector.tensor_copy(out=res_f[:], in_=rp[:, 0:1])

        def turn_words(src32, columns, dst32, copy):
            tu = ring.tile([P, 512], F32, name="tu", tag="ring")
            for u in range(2):
                for r2 in range(2):
                    nc.tensor.transpose(
                        tu[:, 256 * u + 128 * r2 : 256 * u + 128 * r2 + 128], src32(r2)[:, columns(u)], ident_f[:]
                    )
            copy(
                out=dst32.rearrange("p (r u) -> p r u", u=2),
                in_=tu[:].rearrange("p (u r) -> p r u", u=2),
            )

        wg = keep.tile([P, 4 * FEAT], BF16, name="wg", align_bytes=64)
        w_codes = keep.tile([P, FEAT], U32, name="w_codes", align_bytes=64)
        w_sc = keep.tile([P, FEAT], U8, name="w_sc", align_bytes=64)
        hg = keep.tile([P, 4 * NODES], BF16, name="hg", align_bytes=64)
        h_codes = keep.tile([P, NODES], U32, name="h_codes", align_bytes=64)
        h_sc = keep.tile([P, NODES], U8, name="h_sc", align_bytes=64)

        def rows_to_k(src, pair, grouped, copy):
            s32 = src[:].bitcast(F32)
            turn_words(
                lambda r2: s32[:, 256 * (2 * pair + r2) : 256 * (2 * pair + r2) + 256],
                lambda u: slice(128 * u, 128 * u + 128),
                grouped[:].bitcast(F32)[:, 512 * pair : 512 * pair + 512],
                copy,
            )

        def stage0_w():
            rows_to_k(w_sb, 0, wg, nc.scalar.copy)
            rows_to_k(w_sb, 1, wg, nc.vector.tensor_copy)
            nc.vector.quantize_mx(out=w_codes[:].bitcast(FP8X4), scales=w_sc[:], in_=wg[:])

        def stage0_h(g):
            for pair in (2 * g, 2 * g + 1):
                rows_to_k(h_sb, pair, hg, nc.scalar.copy)
            nc.vector.quantize_mx(
                out=h_codes[:, 512 * g : 512 * g + 512].bitcast(FP8X4),
                scales=h_sc[:, 512 * g : 512 * g + 512],
                in_=hg[:, 2048 * g : 2048 * g + 2048],
            )

        hl_t = keep.tile([P, NJ, NODES], BF16, name="hl_t")
        hl_codes = keep.tile([P, NG * FEAT], U32, name="hl_codes", align_bytes=64)
        hl_sc = keep.tile([P, NG * FEAT], U8, name="hl_sc", align_bytes=64)

        def stage1(g):
            for j in range(NJ):
                yb = ypool.tile([P, 512], F32, name="yb", tag="y")
                nc.tensor.matmul_mx(
                    out=yb[:],
                    lhsT=w_codes[:, 128 * j : 128 * j + 128].bitcast(FP8X4),
                    lhsT_scale=w_sc[:, 128 * j : 128 * j + 128],
                    rhs=h_codes[:, 512 * g : 512 * g + 512].bitcast(FP8X4),
                    rhs_scale=h_sc[:, 512 * g : 512 * g + 512],
                    start=True,
                    stop=True,
                )
                nc.scalar.activation(
                    out=hl_t[:, j, 512 * g : 512 * g + 512], in_=yb[:], func=ACT.Identity, bias=gb[:, 8 + j : 9 + j]
                )
            hlg = hlgp.tile([P, 4 * FEAT], BF16, name="hlg", tag="hlg", align_bytes=64)
            for half in range(2):
                turn_words(
                    lambda j2: hl_t[:, 2 * half + j2, :].bitcast(F32),
                    lambda u: slice(256 * g + 128 * u, 256 * g + 128 * u + 128),
                    hlg[:].bitcast(F32)[:, 512 * half : 512 * half + 512],
                    nc.scalar.copy,
                )
            nc.vector.quantize_mx(
                out=hl_codes[:, 512 * g : 512 * g + 512].bitcast(FP8X4),
                scales=hl_sc[:, 512 * g : 512 * g + 512],
                in_=hlg[:],
            )

        zs = keep.tile([P, NJ, NODES], F32, name="zs")
        junk_s = zs[:, 0, 0 : NODES // 2].bitcast(BF16)
        junk_v = zs[:, 1, 0 : NODES // 2].bitcast(BF16)
        deg = const.tile([P, NT], F32, name="deg")
        dis = const.tile([P, NT], F32, name="dis")
        d_sb = keep.tile([P, NODES], F32, name="d_sb")
        adj_i = keep.tile([P, NT, P], F32, name="adj_i")
        dps = {}

        def row_sum(i):
            if i in SCALAR_ROW_SUMS:
                nc.scalar.activation(
                    out=junk_s, in_=a_sb[:, NODES * i : NODES * (i + 1)], func=ACT.Copy, accum_out=deg[:, i : i + 1]
                )
            else:
                nc.vector.tensor_scalar(
                    out=junk_v,
                    in0=a_sb[:, NODES * i : NODES * (i + 1)],
                    scalar1=1.0,
                    scalar2=None,
                    op0=ALU.mult,
                    op1=ALU.add,
                    accum_out=deg[:, i : i + 1],
                )

        def spread(g):
            step = NODES + P
            nc.gpsimd.tensor_tensor(
                out=adj_i[:, 4 * g : 4 * g + 4, :],
                in0=a_sb[:, step * 4 * g : step * (4 * g + 4)].rearrange("q (t x) -> q t x", t=4)[:, :, 0:P],
                in1=ident_f[:].unsqueeze(1).to_broadcast([P, 4, P]),
                op=ALU.add,
            )
            nc.scalar.activation(
                out=dis[:, 4 * g : 4 * g + 4], in_=deg[:, 4 * g : 4 * g + 4], func=ACT.Abs_reciprocal_sqrt, bias=one1[:, 0:1]
            )
            dp = dpool.tile([P, 512], F32, name="dp%d" % g, tag="d%d" % g)
            dps[g] = dp
            for t in range(4):
                nc.tensor.matmul(
                    out=dp[:, 128 * t : 128 * t + 128],
                    lhsT=dis[:, 4 * g + t : 4 * g + t + 1].to_broadcast([P, P]),
                    rhs=ident_f[:],
                    start=True,
                    stop=True,
                )
            nc.scalar.copy(out=d_sb[:, 512 * g : 512 * g + 512], in_=dp[:])

        a_codes = keep.tile([P, NG, NODES], U32, name="a_codes", align_bytes=64)
        a_sc = keep.tile([P, NG, NODES], U8, name="a_sc", align_bytes=64)
        first_tuple = [sum(1 if k in SCALAR_STATS else 2 for k in range(c)) for c in range(LAST + 2)]
        st = const.tile([P, NJ, first_tuple[LAST + 1], 3], F32, name="st")
        for c in SCALAR_STATS:
            nc.vector.memset(st[:, :, first_tuple[c], 0], float(P * CHUNKS[c][1]))
        sums = const.tile([P, LAST, NJ], F32, name="sums")
        negm = const.tile([P, LAST, NJ], F32, name="negm")
        sq = keep.tile([P, 512], F32, name="sq")
        grps, ybs = {}, {}

        def scale_tile(i, g):
            lo = NODES * i + 512 * g
            own = P * (i % 4)
            if i in POOL_ROW_TILES:
                xs = xpool.tile([P, 512], F32, name="xs", tag="xs")
                nc.gpsimd.tensor_scalar(
                    out=xs[:], in0=a_sb[:, lo : lo + 512], scalar1=dis[:, i : i + 1], scalar2=1.0,
                    op0=ALU.mult, op1=ALU.mult,
                )
                if i // 4 == g:
                    nc.gpsimd.tensor_scalar(
                        out=xs[:, own : own + P], in0=adj_i[:, i, :], scalar1=dis[:, i : i + 1], scalar2=1.0,
                        op0=ALU.mult, op1=ALU.mult,
                    )
                nc.gpsimd.tensor_tensor(
                    out=a_sb[:, lo : lo + 512], in0=xs[:], in1=d_sb[:, 512 * g : 512 * g + 512], op=ALU.mult
                )
                return
            nc.vector.scalar_tensor_tensor(
                out=a_sb[:, lo : lo + 512],
                in0=a_sb[:, lo : lo + 512],
                scalar=dis[:, i : i + 1],
                in1=dps[g][:],
                op0=ALU.mult,
                op1=ALU.mult,
            )
            if i // 4 == g:
                nc.vector.scalar_tensor_tensor(
                    out=a_sb[:, lo + own : lo + own + P],
                    in0=adj_i[:, i, :],
                    scalar=dis[:, i : i + 1],
                    in1=dps[g][:, own : own + P],
                    op0=ALU.mult,
                    op1=ALU.mult,
                )

        def unit_front(c, g):
            t0, nt = CHUNKS[c]
            grp = gpool.tile([P, 512 * nt], BF16, name="grp", tag="grp", align_bytes=64)
            grps[(c, g)] = grp
            for i in range(t0, t0 + nt):
                if i in POOL_ROW_TILES:
                    scale_tile(i, g)
            for half in range(nt // 2):
                for i in (t0 + 2 * half, t0 + 2 * half + 1):
                    if i not in POOL_ROW_TILES:
                        scale_tile(i, g)
                turn_words(
                    lambda r2: a32[:, 768 * (t0 + 2 * half + r2) : 768 * (t0 + 2 * half + r2) + 768],
                    lambda u: slice(256 * g + 128 * u, 256 * g + 128 * u + 128),
                    grp[:].bitcast(F32)[:, 512 * half : 512 * half + 512],
                    nc.scalar.copy,
                )

        def nodes_of(c):
            return slice(P * CHUNKS[c][0], P * (CHUNKS[c][0] + CHUNKS[c][1]))

        def unit_quant(c, g):
            nc.vector.quantize_mx(
                out=a_codes[:, g, nodes_of(c)].bitcast(FP8X4), scales=a_sc[:, g, nodes_of(c)], in_=grps[(c, g)][:]
            )

        def one_pass(yb, c, g, j):
            lo = 512 * g + 128 * j
            nc.tensor.matmul_mx(
                out=yb[:],
                lhsT=hl_codes[:, lo : lo + 128].bitcast(FP8X4),
                lhsT_scale=hl_sc[:, lo : lo + 128],
                rhs=a_codes[:, g, nodes_of(c)].bitcast(FP8X4),
                rhs_scale=a_sc[:, g, nodes_of(c)],
                start=(g == 0),
                stop=(g == NG - 1),
            )

        def chunk_matmuls(c):
            for j in range(NJ):
                yb = ypool.tile([P, P * CHUNKS[c][1]], F32, name="yb", tag="y")
                for g in range(NG):
                    one_pass(yb, c, g, j)
                if c in SCALAR_STATS:
                    nc.scalar.activation(
                        out=zs[:, j, nodes_of(c)], in_=yb[:], func=ACT.Copy, accum_out=sums[:, c, j : j + 1]
                    )
                else:
                    nc.scalar.copy(out=zs[:, j, nodes_of(c)], in_=yb[:])

        def chunk_stats(c):
            k = first_tuple[c]
            if c not in SCALAR_STATS:
                for j in range(NJ):
                    nc.vector.bn_stats(
                        out=st[:, j, k : k + 2, :].rearrange("p a b -> p (a b)"),
                        in_=(ybs[j][:] if c == LAST else zs[:, j, nodes_of(c)]),
                    )
                return
            width = P * CHUNKS[c][1]
            nc.scalar.mul(out=negm[:, c, :], in_=sums[:, c, :], mul=-1.0 / width)
            nc.scalar.mul(out=st[:, :, k, 1], in_=sums[:, c, :], mul=1.0 / width)
            for j in range(NJ):
                nc.scalar.activation(
                    out=sq[:, 0:width], in_=zs[:, j, nodes_of(c)], func=ACT.Square, bias=negm[:, c, j : j + 1],
                    accum_out=st[:, j, k, 2:3],
                )

        def last_chunk_banks():
            width = P * CHUNKS[LAST][1]
            ybs[0] = ypool.tile([P, width], F32, name="yb", tag="y")
            ybs[1] = ypool.tile([P, width], F32, name="yb", tag="y")
            ybs[2] = dpool.tile([P, width], F32, name="yd0", tag="d0")
            ybs[3] = dpool.tile([P, width], F32, name="yd1", tag="d1")

        stage0_w()
        stage0_h(0)
        small_vectors()
        stage0_h(1)
        stage0_h(2)
        row_sum(0)
        row_sum(1)
        stage1(0)
        row_sum(2)
        row_sum(3)
        spread(0)
        for i in range(4, 8):
            row_sum(i)
        spread(1)
        for i in range(8, 12):
            row_sum(i)
        spread(2)
        units = [(c, g) for c in range(LAST + 1) for g in range(NG)]
        for k, (c, g) in enumerate(units):
            unit_front(c, g)
            if k in (0, 1):
                stage1(k + 1)
            if k == 0:
                continue
            pc, pg = units[k - 1]
            unit_quant(pc, pg)
            if g == NG - 1 and c > 0:
                chunk_matmuls(c - 1)
                chunk_stats(c - 1)
        last_chunk_banks()
        unit_quant(LAST, NG - 1)
        for g in range(NG):
            for j in range(NJ):
                one_pass(ybs[j], LAST, g, j)
        chunk_stats(LAST)

        mv = const.tile([P, NJ, 2], F32, name="mv")
        for j in range(NJ):
            nc.vector.bn_aggr(out=mv[:, j, :], in_=st[:, j, :, :].rearrange("p c s -> p (c s)"))
        rs = const.tile([P, NJ], F32, name="rs")
        nc.scalar.activation(out=rs[:], in_=mv[:, :, 1], func=ACT.Abs_reciprocal_sqrt, bias=BN_EPS)
        nc.vector.scalar_tensor_tensor(
            out=gn[:, 1, :], in0=mv[:, :, 0], scalar=-1.0, in1=gb[:, 0:4], op0=ALU.mult, op1=ALU.mult
        )
        ss = const.tile([P, 2, NJ], F32, name="ss")
        nc.vector.tensor_tensor(out=ss[:], in0=gn[:], in1=rs[:].unsqueeze(1).to_broadcast([P, 2, NJ]), op=ALU.mult)
        sc = ss[:, 0, :]
        sh = const.tile([P, NJ], F32, name="sh")
        nc.vector.tensor_tensor(out=sh[:], in0=gb[:, 4:8], in1=ss[:, 1, :], op=ALU.add)

        kept = P * CHUNKS[LAST][0]
        for lo, hi in NORMALISE_PIECES:
            for j in range(NJ):
                if lo == 0 and j >= 2:
                    nc.vector.tensor_scalar(
                        out=zs[:, j, lo:hi], in0=zs[:, j, lo:hi], scalar1=sc[:, j : j + 1], scalar2=sh[:, j : j + 1],
                        op0=ALU.mult, op1=ALU.add,
                    )
                    nc.vector.tensor_scalar(
                        out=zs[:, j, lo:hi], in0=zs[:, j, lo:hi], scalar1=0.0, scalar2=None, op0=ALU.max
                    )
                    continue
                nc.scalar.activation(
                    out=zs[:, j, lo:hi],
                    in_=(zs[:, j, lo:hi] if lo < kept else ybs[j][:, lo - kept : hi - kept]),
                    func=ACT.Relu,
                    scale=sc[:, j : j + 1],
                    bias=sh[:, j : j + 1],
                )

        for i in range(NT):
            ob = ring.tile([P, FEAT], F32, name="ob", tag="ring")
            for j in range(NJ):
                nc.tensor.transpose(
                    ob[:, 128 * j : 128 * j + 128], zs[:, j, 128 * i : 128 * i + 128], ident_f[:]
                )
            o_sb = opool.tile([P, FEAT], F32, name="o_sb", tag="o_sb")
            nc.vector.scalar_tensor_tensor(
                out=o_sb[:],
                in0=h_sb[:, 512 * i : 512 * i + 512],
                scalar=res_f[:, 0:1],
                in1=ob[:],
                op0=ALU.mult,
                op1=ALU.add,
            )
            nc.sync.dma_start(out=out_v[:, i, :], in_=o_sb[:])
